import numpy as np
import ml_dtypes


def mxq(x, axis, fmt="e4m3"):
    dtype, down = {"e4m3": (ml_dtypes.float8_e4m3fn, 7), "e5m2": (ml_dtypes.float8_e5m2, 14)}[fmt]
    v = np.moveaxis(np.asarray(x, np.float32).astype(ml_dtypes.bfloat16).astype(np.float64), axis, -1)
    blocks = v.reshape(v.shape[:-1] + (-1, 32))
    amax = np.abs(blocks).max(-1, keepdims=True)
    byte = np.maximum(np.where(amax > 0, np.frexp(amax)[1] - 1 + 127, 0) - down, 1)
    scale = np.exp2(byte - 127.0)
    codes = (blocks / scale).astype(np.float32).astype(dtype).astype(np.float64)
    return np.moveaxis((codes * scale).reshape(v.shape), -1, axis)


WIDE = False


def mx_kscale(k):
    if not WIDE:
        return np.ones(k)
    levels = np.array([10, -10, 5, -5, 0])
    a = np.random.permutation(np.resize(levels, k // 512 * 4)).reshape(k // 512, 4)
    idx = np.arange(k)
    return np.exp2(a[idx // 512, idx % 128 // 32])


BF16 = ml_dtypes.bfloat16


def bf(x):
    return np.asarray(x, np.float32).astype(BF16)


def f64(x):
    return np.asarray(x).astype(np.float64)


E2M1 = np.array([0.0, 0.5, 1.0, 1.5, 2.0, 3.0, 4.0, 6.0, -0.0, -0.5, -1.0, -1.5, -2.0, -3.0, -4.0, -6.0])


def pack_weight(w, fmt):
    k, n = w.shape
    w = f64(bf(w)).reshape(k // 32, 32, n)
    amax = np.abs(w).max(1)
    if fmt == "e4m3":
        byte = np.frexp(amax)[1] - 1 + 127 - 7
    else:
        mant, ex = np.frexp(amax / 6.0)
        byte = np.where(mant > 0.5, ex, ex - 1) + 127
    byte = np.clip(np.where(amax > 0, byte, 1), 1, 254)
    scaled = (w * np.exp2(127.0 - byte)[:, None, :]).reshape(k, n).astype(np.float32)
    by_word = np.ascontiguousarray(scaled.reshape(k // 512, 128, 4, n).transpose(0, 1, 3, 2))
    if fmt == "e4m3":
        words = by_word.astype(ml_dtypes.float8_e4m3fn).view(np.uint8)
    else:
        c = by_word.astype(ml_dtypes.float4_e2m1fn).view(np.uint8) & 0xF
        words = c[..., 0::2] | (c[..., 1::2] << 4)
    return np.ascontiguousarray(words), np.ascontiguousarray(byte.astype(np.uint8).reshape(k // 512, 16, n))


def unpack_weight(words, scales, fmt):
    g, p, n, _ = words.shape
    if fmt == "e4m3":
        vals = np.ascontiguousarray(words).view(ml_dtypes.float8_e4m3fn).astype(np.float64)
    else:
        nib = np.empty((g, p, n, 4), np.uint8)
        nib[..., 0::2] = words & 0xF
        nib[..., 1::2] = words >> 4
        vals = E2M1[nib]
    vals = vals * np.repeat(np.exp2(scales.astype(np.float64) - 127.0), 8, axis=1)[..., None]
    return vals.transpose(0, 1, 3, 2).reshape(g * 512, n)


B, J, C, K, H, M = 8, 128, 512, 4, 8, 256
DH = C // H
S_G2A, S_A2G = 0.5, 0.8
FMT = "e4m3"


def setup_inputs():
    s = mx_kscale(C)
    attn_o = bf(np.random.standard_normal((B, H, J, DH)) * 0.6 * s.reshape(H, 1, DH))
    xg1 = bf(np.random.standard_normal((B, J, C)) * 0.7 * s)
    x = bf(np.random.standard_normal((B, J, C)))
    adj = bf(np.random.uniform(size=(K, J, J)) / np.sqrt(K * J))
    proj_w_words, proj_w_scales = pack_weight((np.random.standard_normal((C, C)) / np.sqrt(C) / s).T, FMT)
    proj_b = bf(0.1 * np.random.standard_normal(C))
    gcn2_w_words, gcn2_w_scales = pack_weight((np.random.standard_normal((K * C, C)) * 1.5 / np.sqrt(C) / s).T, FMT)
    gcn2_b = bf(np.random.standard_normal(K * C) * 0.6 / np.sqrt(J))
    return {'attn_o': attn_o,
            'xg1': xg1,
            'x': x,
            'adj': adj,
            'proj_w_words': proj_w_words,
            'proj_w_scales': proj_w_scales,
            'proj_b': proj_b,
            'gcn2_w_words': gcn2_w_words,
            'gcn2_w_scales': gcn2_w_scales,
            'gcn2_b': gcn2_b}


def reference(attn_o, xg1, x, adj, proj_w_words, proj_w_scales, proj_b, gcn2_w_words, gcn2_w_scales, gcn2_b):
    o = f64(attn_o)
    g1 = f64(xg1)
    attn2gcn = o.transpose(0, 2, 1, 3).reshape(B, J, C)
    fh = (g1 * S_G2A).reshape(B, J, H, DH).transpose(0, 2, 1, 3)
    v = (o + fh).transpose(0, 2, 1, 3).reshape(B, J, C)
    xa = (mxq(v, 2, 'e4m3') @ unpack_weight(proj_w_words, proj_w_scales, FMT)) + f64(proj_b)
    u = g1 + attn2gcn * S_A2G
    y = (mxq(u, 2, 'e4m3') @ unpack_weight(gcn2_w_words, gcn2_w_scales, FMT)) + f64(gcn2_b)
    yk = y.reshape(B, J, K, C).transpose(0, 2, 1, 3).reshape(B, K * J, C)
    a = f64(adj).reshape(K * J, J)
    xg2 = mxq(a, 0, 'e4m3').T @ mxq(yk, 1, 'e4m3')
    return f64(x) + xg2 + xa

@@ -1,0 +1,249 @@
+from contextlib import ExitStack
+
+import concourse.mybir as mybir
+from concourse.masks import make_identity
+
+BF16 = mybir.dt.bfloat16
+F32 = mybir.dt.float32
+I32 = mybir.dt.int32
+U32 = mybir.dt.uint32
+U8 = mybir.dt.uint8
+FP8X4 = mybir.dt.float8_e4m3fn_x4
+ADD = mybir.AluOpType.add
+MULT = mybir.AluOpType.mult
+
+P = 128
+PACK = 4
+B = 8
+H = 8
+DH = 64
+C = 512
+K = 4
+CHUNK = 128
+N_CHUNKS = C // CHUNK
+S_G2A = 0.5
+S_A2G = 0.8
+AHEAD = 2
+
+FLOPS = 2 * B * P * C * C + 2 * B * P * C * K * C + 2 * B * P * K * P * C
+
+
+def tile_block_pb_kernel(
+    tc,
+    attn_o,
+    xg1,
+    x,
+    adj,
+    proj_w_words,
+    proj_w_scales,
+    proj_b,
+    gcn2_w_words,
+    gcn2_w_scales,
+    gcn2_b,
+    out,
+):
+    nc = tc.nc
+    with ExitStack() as ctx:
+        keep = ctx.enter_context(tc.tile_pool(name="keep", bufs=1))
+        work = ctx.enter_context(tc.tile_pool(name="work", bufs=2))
+        ps_t = ctx.enter_context(tc.psum_pool(name="ps_t", bufs=2))
+        ps_y = ctx.enter_context(tc.psum_pool(name="ps_y", bufs=N_CHUNKS))
+        ps_x = ctx.enter_context(tc.psum_pool(name="ps_x", bufs=1))
+        ps_o = ctx.enter_context(tc.psum_pool(name="ps_o", bufs=1))
+
+        a_sb = keep.tile([P, B, C], BF16)
+        g_sb = keep.tile([P, B, C], BF16)
+        x_sb = keep.tile([P, B, C], BF16)
+        adj_sb = keep.tile([P, K, P], BF16)
+        gcn2_words = keep.tile([P, K * C], U32, align_bytes=64)
+        proj_words = keep.tile([P, C], U32, align_bytes=64)
+        gcn2_plane = keep.tile([P, K * C], U8, align_bytes=64)
+        proj_plane = keep.tile([P, C], U8, align_bytes=64)
+        bias_rows = keep.tile([P, K, C], BF16)
+        bias_ck = keep.tile([P, C, K], F32)
+        projb_row = keep.tile([P, C], BF16)
+        ones = keep.tile([P, P], BF16)
+        ident_f32 = keep.tile([P, P], F32)
+        ident_bf16 = keep.tile([P, P], BF16)
+        ag_t = keep.tile([P, B, 2, C], BF16)
+        half_g_t = keep.tile([P, B, C], BF16)
+        uv_words = keep.tile([P, B, 2 * P], U32, align_bytes=64)
+        uv_plane = keep.tile([P, B, 2 * P], U8, align_bytes=64)
+        adj_kw = keep.tile([P, P, K], BF16, align_bytes=64)
+        adj_words = keep.tile([P, P], U32, align_bytes=64)
+        adj_plane = keep.tile([P, P], U8, align_bytes=64)
+        xpb = keep.tile([P, B, C], F32)
+
+        nc.vector.memset(gcn2_plane[:].bitcast(I32), 0)
+        nc.vector.memset(proj_plane[:].bitcast(I32), 0)
+        nc.vector.memset(projb_row[:], 0.0)
+        nc.vector.memset(ones[:], 1.0)
+        make_identity(nc, ident_f32[:])
+        make_identity(nc, ident_bf16[:])
+
+        def load_streams(b):
+            nc.sync.dma_start(
+                out=a_sb[:, b, :].rearrange("j (h d) -> j h d", h=H),
+                in_=attn_o[b].rearrange("h j d -> j h d"),
+            )
+            nc.sync.dma_start(out=g_sb[:, b, :], in_=xg1[b])
+
+        def load_scales(plane, scales):
+            for r in range(4):
+                nc.sync.dma_start(
+                    out=plane[r:P:32, :].bitcast(I32), in_=scales[0, r:16:4, :].bitcast(I32)
+                )
+
+        load_streams(0)
+        load_scales(gcn2_plane, gcn2_w_scales)
+        gcn2_dram = gcn2_w_words[0].rearrange("p n t -> p (n t)").bitcast(I32)
+        for n in range(N_CHUNKS):
+            cols = slice(n * CHUNK, (n + 1) * CHUNK)
+            nc.sync.dma_start(
+                out=gcn2_words[:].bitcast(I32).rearrange("p (k c) -> p k c", k=K)[:, :, cols],
+                in_=gcn2_dram.rearrange("p (k c) -> p k c", k=K)[:, :, cols],
+            )
+        nc.sync.dma_start(
+            out=bias_rows[:].rearrange("p k c -> p (k c)"), in_=gcn2_b.partition_broadcast(P)
+        )
+        load_streams(1)
+        nc.sync.dma_start(out=adj_sb[:], in_=adj.rearrange("k j w -> j k w"))
+        load_scales(proj_plane, proj_w_scales)
+        nc.sync.dma_start(
+            out=proj_words[:].bitcast(I32),
+            in_=proj_w_words[0].rearrange("p n t -> p (n t)").bitcast(I32),
+        )
+        nc.sync.dma_start(out=projb_row[0:1, :], in_=proj_b.unsqueeze(0))
+        nc.sync.dma_start(out=x_sb[:], in_=x.rearrange("b j c -> j b c"))
+        for b in range(2, B):
+            load_streams(b)
+
+        nc.vector.tensor_copy(out=bias_ck[:], in_=bias_rows[:].rearrange("p k c -> p c k"))
+
+        nc.vector.tensor_copy(out=adj_kw[:], in_=adj_sb[:].rearrange("p k w -> p w k"))
+        nc.vector.quantize_mx(
+            out=adj_words[:].bitcast(FP8X4),
+            scales=adj_plane[:],
+            in_=adj_kw[:].rearrange("p w k -> p (w k)"),
+        )
+
+        def transpose_streams(b):
+            turned = ps_t.tile([P, 4, P], F32)
+            for which, src in enumerate((a_sb, g_sb)):
+                for half in range(2):
+                    nc.tensor.transpose(
+                        out=turned[:, 2 * which + half, :],
+                        in_=src[:, b, :].bitcast(F32)[:, half : C // 2 : 2],
+                        identity=ident_f32[:],
+                    )
+            nc.scalar.copy(
+                out=ag_t[:, b].bitcast(F32).rearrange("p x (j h) -> p x j h", h=2),
+                in_=turned[:].rearrange("p (x h) j -> p x j h", h=2),
+            )
+            nc.scalar.mul(
+                out=half_g_t[:, b, :].rearrange("p (j h e) -> p j h e", h=2, e=2),
+                in_=turned[:, 2:4, :].bitcast(BF16).rearrange("p h (j e) -> p j h e", e=2),
+                mul=S_G2A,
+            )
+
+        def mix_streams(b):
+            uv = work.tile([P, 2, C], BF16, align_bytes=64)
+            nc.vector.tensor_tensor(
+                out=uv[:, 0, :], in0=ag_t[:, b, 0, :], in1=half_g_t[:, b, :], op=ADD
+            )
+            nc.vector.scalar_tensor_tensor(
+                out=uv[:, 1, :], in0=ag_t[:, b, 0, :], scalar=S_A2G, in1=ag_t[:, b, 1, :],
+                op0=MULT, op1=ADD,
+            )
+            return uv
+
+        def quantise_streams(b, uv):
+            nc.vector.quantize_mx(
+                out=uv_words[:, b, :].bitcast(FP8X4),
+                scales=uv_plane[:, b, :],
+                in_=uv[:].rearrange("p s c -> p (s c)"),
+            )
+
+        def graph_matmul(b, n):
+            bank = ps_y.tile([P, K, CHUNK], F32)
+            for k in range(K):
+                cols = slice(k * C + n * CHUNK, k * C + (n + 1) * CHUNK)
+                nc.tensor.matmul_mx(
+                    out=bank[:, k, :],
+                    lhsT=uv_words[:, b, P : 2 * P].bitcast(FP8X4),
+                    lhsT_scale=uv_plane[:, b, P : 2 * P],
+                    rhs=gcn2_words[:, cols].bitcast(FP8X4),
+                    rhs_scale=gcn2_plane[:, cols],
+                    start=True,
+                    stop=True,
+                )
+            return bank
+
+        def residual(b):
+            acc = ps_x.tile([P, C], F32)
+            nc.tensor.matmul(out=acc[:], lhsT=ident_bf16[:], rhs=x_sb[:, b, :], start=True, stop=False)
+            nc.tensor.matmul(out=acc[:], lhsT=ones[:], rhs=projb_row[:], start=False, stop=True)
+            nc.scalar.copy(out=xpb[:, b, :], in_=acc[:])
+
+        def output_matmul(b, y_words, y_plane):
+            acc = ps_o.tile([P, C], F32)
+            nc.tensor.matmul_mx(
+                out=acc[:],
+                lhsT=uv_words[:, b, 0:P].bitcast(FP8X4),
+                lhsT_scale=uv_plane[:, b, 0:P],
+                rhs=proj_words[:].bitcast(FP8X4),
+                rhs_scale=proj_plane[:],
+                start=True,
+                stop=False,
+            )
+            nc.tensor.matmul_mx(
+                out=acc[:],
+                lhsT=adj_words[:].bitcast(FP8X4),
+                lhsT_scale=adj_plane[:],
+                rhs=y_words[:].bitcast(FP8X4),
+                rhs_scale=y_plane[:],
+                start=False,
+                stop=True,
+            )
+            return acc
+
+        def finish(b, acc):
+            result = work.tile([P, C], F32)
+            nc.vector.tensor_tensor(out=result[:], in0=acc[:], in1=xpb[:, b, :], op=ADD)
+            nc.sync.dma_start(out=out[b], in_=result[:])
+
+        for b in range(AHEAD):
+            transpose_streams(b)
+            quantise_streams(b, mix_streams(b))
+        banks = [graph_matmul(0, n) for n in range(N_CHUNKS)]
+        pending = None
+        for b in range(B):
+            if b + AHEAD < B:
+                transpose_streams(b + AHEAD)
+            residual(b)
+            y_ck = work.tile([P, C, K], BF16, align_bytes=64)
+            for n in range(N_CHUNKS):
+                cols = slice(n * CHUNK, (n + 1) * CHUNK)
+                nc.vector.tensor_tensor(
+                    out=y_ck[:, cols, :],
+                    in0=banks[n][:].rearrange("p k c -> p c k"),
+                    in1=bias_ck[:, cols, :],
+                    op=ADD,
+                )
+                if b + 1 < B:
+                    banks[n] = graph_matmul(b + 1, n)
+            if pending is not None:
+                finish(b - 1, pending)
+            if b + AHEAD < B:
+                uv_next = mix_streams(b + AHEAD)
+            y_words = work.tile([P, C], U32, align_bytes=64)
+            y_plane = work.tile([P, C], U8, align_bytes=64)
+            nc.vector.quantize_mx(
+                out=y_words[:].bitcast(FP8X4),
+                scales=y_plane[:],
+                in_=y_ck[:].rearrange("p c k -> p (c k)"),
+            )
+            if b + AHEAD < B:
+                quantise_streams(b + AHEAD, uv_next)
+            pending = output_matmul(b, y_words, y_plane)
+        finish(B - 1, pending)

@@ -48,8 +48,8 @@ def tile_block_pb_kernel(
         work = ctx.enter_context(tc.tile_pool(name="work", bufs=2))
         ps_t = ctx.enter_context(tc.psum_pool(name="ps_t", bufs=2))
         ps_y = ctx.enter_context(tc.psum_pool(name="ps_y", bufs=N_CHUNKS))
-        ps_x = ctx.enter_context(tc.psum_pool(name="ps_x", bufs=1))
-        ps_o = ctx.enter_context(tc.psum_pool(name="ps_o", bufs=1))
+        ps_o = ctx.enter_context(tc.psum_pool(name="ps_o", bufs=2))
+        ctx.enter_context(tc.manual_schedule())
 
         a_sb = keep.tile([P, B, C], BF16)
         g_sb = keep.tile([P, B, C], BF16)
@@ -59,12 +59,11 @@ def tile_block_pb_kernel(
         proj_words = keep.tile([P, C], U32, align_bytes=64)
         gcn2_plane = keep.tile([P, K * C], U8, align_bytes=64)
         proj_plane = keep.tile([P, C], U8, align_bytes=64)
-        bias_rows = keep.tile([P, K, C], BF16)
-        bias_ck = keep.tile([P, C, K], F32)
-        projb_row = keep.tile([P, C], BF16)
+        bias_row = keep.tile([P, K * C + C], BF16)
         ones = keep.tile([P, P], BF16)
+        bias_ck = keep.tile([P, C, K], F32)
+        projb_all = keep.tile([P, C], F32)
         ident_f32 = keep.tile([P, P], F32)
-        ident_bf16 = keep.tile([P, P], BF16)
         ag_t = keep.tile([P, B, 2, C], BF16)
         half_g_t = keep.tile([P, B, C], BF16)
         uv_words = keep.tile([P, B, 2 * P], U32, align_bytes=64)
@@ -74,12 +73,14 @@ def tile_block_pb_kernel(
         adj_plane = keep.tile([P, P], U8, align_bytes=64)
         xpb = keep.tile([P, B, C], F32)
 
+        nc.vector.memset(bias_row[:].bitcast(I32), 0)
         nc.vector.memset(gcn2_plane[:].bitcast(I32), 0)
         nc.vector.memset(proj_plane[:].bitcast(I32), 0)
-        nc.vector.memset(projb_row[:], 0.0)
         nc.vector.memset(ones[:], 1.0)
         make_identity(nc, ident_f32[:])
-        make_identity(nc, ident_bf16[:])
+
+        nc.scalar.dma_start(out=bias_row[0:1, 0 : K * C], in_=gcn2_b.unsqueeze(0))
+        nc.scalar.dma_start(out=bias_row[0:1, K * C : K * C + C], in_=proj_b.unsqueeze(0))
 
         def load_streams(b):
             nc.sync.dma_start(
@@ -94,38 +95,42 @@ def tile_block_pb_kernel(
                     out=plane[r:P:32, :].bitcast(I32), in_=scales[0, r:16:4, :].bitcast(I32)
                 )
 
-        load_streams(0)
-        load_scales(gcn2_plane, gcn2_w_scales)
-        gcn2_dram = gcn2_w_words[0].rearrange("p n t -> p (n t)").bitcast(I32)
-        for n in range(N_CHUNKS):
-            cols = slice(n * CHUNK, (n + 1) * CHUNK)
+        def load_words(words, dram):
             nc.sync.dma_start(
-                out=gcn2_words[:].bitcast(I32).rearrange("p (k c) -> p k c", k=K)[:, :, cols],
-                in_=gcn2_dram.rearrange("p (k c) -> p k c", k=K)[:, :, cols],
+                out=words[:].bitcast(I32), in_=dram[0].rearrange("p n t -> p (n t)").bitcast(I32)
             )
-        nc.sync.dma_start(
-            out=bias_rows[:].rearrange("p k c -> p (k c)"), in_=gcn2_b.partition_broadcast(P)
-        )
-        load_streams(1)
+
+        for b in range(AHEAD):
+            load_streams(b)
+        load_scales(gcn2_plane, gcn2_w_scales)
+        load_words(gcn2_words, gcn2_w_words)
+        load_streams(AHEAD)
         nc.sync.dma_start(out=adj_sb[:], in_=adj.rearrange("k j w -> j k w"))
         load_scales(proj_plane, proj_w_scales)
-        nc.sync.dma_start(
-            out=proj_words[:].bitcast(I32),
-            in_=proj_w_words[0].rearrange("p n t -> p (n t)").bitcast(I32),
-        )
-        nc.sync.dma_start(out=projb_row[0:1, :], in_=proj_b.unsqueeze(0))
-        nc.sync.dma_start(out=x_sb[:], in_=x.rearrange("b j c -> j b c"))
-        for b in range(2, B):
-            load_streams(b)
+        load_words(proj_words, proj_w_words)
+        for b in range(B):
+            nc.sync.dma_start(out=x_sb[:, b, :], in_=x[b])
+            if b + AHEAD + 1 < B:
+                load_streams(b + AHEAD + 1)
 
-        nc.vector.tensor_copy(out=bias_ck[:], in_=bias_rows[:].rearrange("p k c -> p c k"))
+        def spread_bias(n):
+            bank = ps_y.tile([P, K, CHUNK], F32)
+            for k in range(K):
+                cols = slice(k * C + n * CHUNK, k * C + (n + 1) * CHUNK)
+                nc.tensor.matmul(
+                    out=bank[:, k, :], lhsT=ones[:], rhs=bias_row[:, cols], start=True, stop=True
+                )
+            nc.scalar.copy(
+                out=bias_ck[:, n * CHUNK : (n + 1) * CHUNK, :],
+                in_=bank[:].rearrange("p k c -> p c k"),
+            )
 
-        nc.vector.tensor_copy(out=adj_kw[:], in_=adj_sb[:].rearrange("p k w -> p w k"))
-        nc.vector.quantize_mx(
-            out=adj_words[:].bitcast(FP8X4),
-            scales=adj_plane[:],
-            in_=adj_kw[:].rearrange("p w k -> p (w k)"),
-        )
+        def spread_proj_bias():
+            acc = ps_o.tile([P, C], F32)
+            nc.tensor.matmul(
+                out=acc[:], lhsT=ones[:], rhs=bias_row[:, K * C : K * C + C], start=True, stop=True
+            )
+            nc.scalar.copy(out=projb_all[:], in_=acc[:])
 
         def transpose_streams(b):
             turned = ps_t.tile([P, 4, P], F32)
@@ -148,12 +153,12 @@ def tile_block_pb_kernel(
 
         def mix_streams(b):
             uv = work.tile([P, 2, C], BF16, align_bytes=64)
-            nc.vector.tensor_tensor(
-                out=uv[:, 0, :], in0=ag_t[:, b, 0, :], in1=half_g_t[:, b, :], op=ADD
-            )
             nc.vector.scalar_tensor_tensor(
                 out=uv[:, 1, :], in0=ag_t[:, b, 0, :], scalar=S_A2G, in1=ag_t[:, b, 1, :],
                 op0=MULT, op1=ADD,
+            )
+            nc.vector.tensor_tensor(
+                out=uv[:, 0, :], in0=ag_t[:, b, 0, :], in1=half_g_t[:, b, :], op=ADD
             )
             return uv
 
@@ -162,6 +167,14 @@ def tile_block_pb_kernel(
                 out=uv_words[:, b, :].bitcast(FP8X4),
                 scales=uv_plane[:, b, :],
                 in_=uv[:].rearrange("p s c -> p (s c)"),
+            )
+
+        def quantise_adjacency():
+            nc.scalar.copy(out=adj_kw[:], in_=adj_sb[:].rearrange("p k w -> p w k"))
+            nc.vector.quantize_mx(
+                out=adj_words[:].bitcast(FP8X4),
+                scales=adj_plane[:],
+                in_=adj_kw[:].rearrange("p w k -> p (w k)"),
             )
 
         def graph_matmul(b, n):
@@ -178,12 +191,6 @@ def tile_block_pb_kernel(
                     stop=True,
                 )
             return bank
-
-        def residual(b):
-            acc = ps_x.tile([P, C], F32)
-            nc.tensor.matmul(out=acc[:], lhsT=ident_bf16[:], rhs=x_sb[:, b, :], start=True, stop=False)
-            nc.tensor.matmul(out=acc[:], lhsT=ones[:], rhs=projb_row[:], start=False, stop=True)
-            nc.scalar.copy(out=xpb[:, b, :], in_=acc[:])
 
         def output_matmul(b, y_words, y_plane):
             acc = ps_o.tile([P, C], F32)
@@ -212,15 +219,22 @@ def tile_block_pb_kernel(
             nc.vector.tensor_tensor(out=result[:], in0=acc[:], in1=xpb[:, b, :], op=ADD)
             nc.sync.dma_start(out=out[b], in_=result[:])
 
+        spread_bias(0)
+        first = []
         for b in range(AHEAD):
             transpose_streams(b)
-            quantise_streams(b, mix_streams(b))
+            first.append(mix_streams(b))
+        for n in range(1, N_CHUNKS):
+            spread_bias(n)
+        spread_proj_bias()
+        for b in range(AHEAD):
+            quantise_streams(b, first[b])
         banks = [graph_matmul(0, n) for n in range(N_CHUNKS)]
         pending = None
         for b in range(B):
             if b + AHEAD < B:
                 transpose_streams(b + AHEAD)
-            residual(b)
+            nc.gpsimd.tensor_tensor(out=xpb[:, b, :], in0=x_sb[:, b, :], in1=projb_all[:], op=ADD)
             y_ck = work.tile([P, C, K], BF16, align_bytes=64)
             for n in range(N_CHUNKS):
                 cols = slice(n * CHUNK, (n + 1) * CHUNK)
@@ -245,5 +259,7 @@ def tile_block_pb_kernel(
             )
             if b + AHEAD < B:
                 quantise_streams(b + AHEAD, uv_next)
+            if b == 0:
+                quantise_adjacency()
             pending = output_matmul(b, y_words, y_plane)
         finish(B - 1, pending)

@@ -11,19 +11,20 @@ U8 = mybir.dt.uint8
 FP8X4 = mybir.dt.float8_e4m3fn_x4
 ADD = mybir.AluOpType.add
 MULT = mybir.AluOpType.mult
+IDENTITY = mybir.ActivationFunctionType.Identity
 
 P = 128
-PACK = 4
 B = 8
 H = 8
-DH = 64
 C = 512
 K = 4
 CHUNK = 128
 N_CHUNKS = C // CHUNK
+N_DIRECT = 2
+N_TURNED = N_CHUNKS - N_DIRECT
+C_DIRECT = N_DIRECT * CHUNK
 S_G2A = 0.5
 S_A2G = 0.8
-AHEAD = 2
 
 FLOPS = 2 * B * P * C * C + 2 * B * P * C * K * C + 2 * B * P * K * P * C
 
@@ -47,39 +48,50 @@ def tile_block_pb_kernel(
         keep = ctx.enter_context(tc.tile_pool(name="keep", bufs=1))
         work = ctx.enter_context(tc.tile_pool(name="work", bufs=2))
         ps_t = ctx.enter_context(tc.psum_pool(name="ps_t", bufs=2))
-        ps_y = ctx.enter_context(tc.psum_pool(name="ps_y", bufs=N_CHUNKS))
-        ps_o = ctx.enter_context(tc.psum_pool(name="ps_o", bufs=2))
+        ps_yd = ctx.enter_context(tc.psum_pool(name="ps_yd", bufs=N_DIRECT))
+        ps_yt = ctx.enter_context(tc.psum_pool(name="ps_yt", bufs=N_TURNED))
+        ps_r = ctx.enter_context(tc.psum_pool(name="ps_r", bufs=1))
+        ps_o = ctx.enter_context(tc.psum_pool(name="ps_o", bufs=1))
         ctx.enter_context(tc.manual_schedule())
 
         a_sb = keep.tile([P, B, C], BF16)
         g_sb = keep.tile([P, B, C], BF16)
         x_sb = keep.tile([P, B, C], BF16)
         adj_sb = keep.tile([P, K, P], BF16)
+        adj2_sb = keep.tile([P, K, P], BF16)
         gcn2_words = keep.tile([P, K * C], U32, align_bytes=64)
         proj_words = keep.tile([P, C], U32, align_bytes=64)
         gcn2_plane = keep.tile([P, K * C], U8, align_bytes=64)
         proj_plane = keep.tile([P, C], U8, align_bytes=64)
         bias_row = keep.tile([P, K * C + C], BF16)
+        bias_rows = keep.tile([P, P], BF16)
         ones = keep.tile([P, P], BF16)
-        bias_ck = keep.tile([P, C, K], F32)
+        bias_ck = keep.tile([P, C_DIRECT, K], F32)
+        bias_col = keep.tile([P, K * N_CHUNKS], F32)
         projb_all = keep.tile([P, C], F32)
         ident_f32 = keep.tile([P, P], F32)
+        ident_bf = keep.tile([P, P], BF16)
         ag_t = keep.tile([P, B, 2, C], BF16)
         half_g_t = keep.tile([P, B, C], BF16)
         uv_words = keep.tile([P, B, 2 * P], U32, align_bytes=64)
         uv_plane = keep.tile([P, B, 2 * P], U8, align_bytes=64)
-        adj_kw = keep.tile([P, P, K], BF16, align_bytes=64)
-        adj_words = keep.tile([P, P], U32, align_bytes=64)
-        adj_plane = keep.tile([P, P], U8, align_bytes=64)
+        adj_kw = keep.tile([P, 2, P, K], BF16, align_bytes=64)
+        adj_words = keep.tile([P, 2, P], U32, align_bytes=64)
+        adj_plane = keep.tile([P, 2, P], U8, align_bytes=64)
         xpb = keep.tile([P, B, C], F32)
 
         nc.vector.memset(bias_row[:].bitcast(I32), 0)
+        nc.vector.memset(bias_rows[:].bitcast(I32), 0)
         nc.vector.memset(gcn2_plane[:].bitcast(I32), 0)
         nc.vector.memset(proj_plane[:].bitcast(I32), 0)
         nc.vector.memset(ones[:], 1.0)
         make_identity(nc, ident_f32[:])
+        make_identity(nc, ident_bf[:])
 
         nc.scalar.dma_start(out=bias_row[0:1, 0 : K * C], in_=gcn2_b.unsqueeze(0))
+        nc.scalar.dma_start(
+            out=bias_rows[0 : K * N_CHUNKS, :], in_=gcn2_b.rearrange("(q c) -> q c", c=CHUNK)
+        )
         nc.scalar.dma_start(out=bias_row[0:1, K * C : K * C + C], in_=proj_b.unsqueeze(0))
 
         def load_streams(b):
@@ -100,21 +112,26 @@ def tile_block_pb_kernel(
                 out=words[:].bitcast(I32), in_=dram[0].rearrange("p n t -> p (n t)").bitcast(I32)
             )
 
-        for b in range(AHEAD):
-            load_streams(b)
+        load_streams(0)
+        load_streams(1)
         load_scales(gcn2_plane, gcn2_w_scales)
         load_words(gcn2_words, gcn2_w_words)
-        load_streams(AHEAD)
+        load_streams(2)
+        load_streams(3)
         nc.sync.dma_start(out=adj_sb[:], in_=adj.rearrange("k j w -> j k w"))
+        nc.sync.dma_start(
+            out=adj2_sb[:].rearrange("p (u e) w -> p u e w", u=2),
+            in_=adj.rearrange("k j w -> (k j) w").rearrange("(u p e) w -> p u e w", u=2, e=2),
+        )
         load_scales(proj_plane, proj_w_scales)
         load_words(proj_words, proj_w_words)
         for b in range(B):
+            if b + 4 < B:
+                load_streams(b + 4)
             nc.sync.dma_start(out=x_sb[:, b, :], in_=x[b])
-            if b + AHEAD + 1 < B:
-                load_streams(b + AHEAD + 1)
 
         def spread_bias(n):
-            bank = ps_y.tile([P, K, CHUNK], F32)
+            bank = ps_yd.tile([P, K, CHUNK], F32, name="bank_d")
             for k in range(K):
                 cols = slice(k * C + n * CHUNK, k * C + (n + 1) * CHUNK)
                 nc.tensor.matmul(
@@ -125,15 +142,20 @@ def tile_block_pb_kernel(
                 in_=bank[:].rearrange("p k c -> p c k"),
             )
 
+        def turn_bias():
+            turned_bias = ps_r.tile([P, P], BF16, name="bank_r")
+            nc.tensor.transpose(out=turned_bias[:], in_=bias_rows[:], identity=ident_bf[:])
+            nc.scalar.copy(out=bias_col[:], in_=turned_bias[:, 0 : K * N_CHUNKS])
+
         def spread_proj_bias():
-            acc = ps_o.tile([P, C], F32)
+            acc = ps_o.tile([P, C], F32, name="acc")
             nc.tensor.matmul(
                 out=acc[:], lhsT=ones[:], rhs=bias_row[:, K * C : K * C + C], start=True, stop=True
             )
             nc.scalar.copy(out=projb_all[:], in_=acc[:])
 
         def transpose_streams(b):
-            turned = ps_t.tile([P, 4, P], F32)
+            turned = ps_t.tile([P, 4, P], F32, name="turned")
             for which, src in enumerate((a_sb, g_sb)):
                 for half in range(2):
                     nc.tensor.transpose(
@@ -141,10 +163,15 @@ def tile_block_pb_kernel(
                         in_=src[:, b, :].bitcast(F32)[:, half : C // 2 : 2],
                         identity=ident_f32[:],
                     )
+            return turned
+
+        def copy_streams(b, turned):
             nc.scalar.copy(
                 out=ag_t[:, b].bitcast(F32).rearrange("p x (j h) -> p x j h", h=2),
                 in_=turned[:].rearrange("p (x h) j -> p x j h", h=2),
             )
+
+        def halve_stream(b, turned):
             nc.scalar.mul(
                 out=half_g_t[:, b, :].rearrange("p (j h e) -> p j h e", h=2, e=2),
                 in_=turned[:, 2:4, :].bitcast(BF16).rearrange("p h (j e) -> p j h e", e=2),
@@ -152,7 +179,7 @@ def tile_block_pb_kernel(
             )
 
         def mix_streams(b):
-            uv = work.tile([P, 2, C], BF16, align_bytes=64)
+            uv = work.tile([P, 2, C], BF16, align_bytes=64, name="uv")
             nc.vector.scalar_tensor_tensor(
                 out=uv[:, 1, :], in0=ag_t[:, b, 0, :], scalar=S_A2G, in1=ag_t[:, b, 1, :],
                 op0=MULT, op1=ADD,
@@ -169,16 +196,19 @@ def tile_block_pb_kernel(
                 in_=uv[:].rearrange("p s c -> p (s c)"),
             )
 
+        def interleave_adjacency():
+            nc.scalar.copy(out=adj_kw[:, 0], in_=adj_sb[:].rearrange("p k w -> p w k"))
+            nc.scalar.copy(out=adj_kw[:, 1], in_=adj2_sb[:].rearrange("p k w -> p w k"))
+
         def quantise_adjacency():
-            nc.scalar.copy(out=adj_kw[:], in_=adj_sb[:].rearrange("p k w -> p w k"))
             nc.vector.quantize_mx(
-                out=adj_words[:].bitcast(FP8X4),
-                scales=adj_plane[:],
-                in_=adj_kw[:].rearrange("p w k -> p (w k)"),
+                out=adj_words[:].rearrange("p s w -> p (s w)").bitcast(FP8X4),
+                scales=adj_plane[:].rearrange("p s w -> p (s w)"),
+                in_=adj_kw[:].rearrange("p s w k -> p (s w k)"),
             )
 
-        def graph_matmul(b, n):
-            bank = ps_y.tile([P, K, CHUNK], F32)
+        def direct_matmul(b, n):
+            bank = ps_yd.tile([P, K, CHUNK], F32, name="bank_d")
             for k in range(K):
                 cols = slice(k * C + n * CHUNK, k * C + (n + 1) * CHUNK)
                 nc.tensor.matmul_mx(
@@ -192,74 +222,152 @@ def tile_block_pb_kernel(
                 )
             return bank
 
+        def turned_matmul(b, n):
+            bank = ps_yt.tile([P, K, P], F32, name="bank_t")
+            for k in range(K):
+                cols = slice(k * C + n * CHUNK, k * C + (n + 1) * CHUNK)
+                nc.tensor.matmul_mx(
+                    out=bank[:, k, :],
+                    lhsT=gcn2_words[:, cols].bitcast(FP8X4),
+                    lhsT_scale=gcn2_plane[:, cols],
+                    rhs=uv_words[:, b, P : 2 * P].bitcast(FP8X4),
+                    rhs_scale=uv_plane[:, b, P : 2 * P],
+                    start=True,
+                    stop=True,
+                )
+            return bank
+
+        def direct_bias(y_ck, n, bank):
+            cols = slice(n * CHUNK, (n + 1) * CHUNK)
+            nc.vector.tensor_tensor(
+                out=y_ck[:, cols, :],
+                in0=bank[:].rearrange("p k c -> p c k"),
+                in1=bias_ck[:, cols, :],
+                op=ADD,
+            )
+
+        def turned_bias_add(y_t, n, bank):
+            for k in range(K):
+                q = k * N_CHUNKS + n
+                nc.scalar.activation(
+                    out=y_t[:, n - N_DIRECT, k, :],
+                    in_=bank[:, k, :],
+                    func=IDENTITY,
+                    bias=bias_col[:, q : q + 1],
+                )
+
+        def turn_back(y_t):
+            back = ps_r.tile([P, N_TURNED, 2, P], F32, name="bank_r")
+            for i in range(N_TURNED):
+                words = y_t[:, i].rearrange("p k j -> p (k j)").bitcast(F32)
+                for u in range(2):
+                    nc.tensor.transpose(
+                        out=back[:, i, u, :], in_=words[:, u * P : (u + 1) * P], identity=ident_f32[:]
+                    )
+            return back
+
+        def copy_back(y_ck, back):
+            nc.scalar.copy(
+                out=y_ck[:, C_DIRECT:C, :]
+                .rearrange("p c k -> p (c k)")
+                .bitcast(F32)
+                .rearrange("p (i c u) -> p i c u", i=N_TURNED, u=2),
+                in_=back[:].rearrange("p i u c -> p i c u"),
+            )
+
         def output_matmul(b, y_words, y_plane):
-            acc = ps_o.tile([P, C], F32)
-            nc.tensor.matmul_mx(
-                out=acc[:],
-                lhsT=uv_words[:, b, 0:P].bitcast(FP8X4),
-                lhsT_scale=uv_plane[:, b, 0:P],
-                rhs=proj_words[:].bitcast(FP8X4),
-                rhs_scale=proj_plane[:],
-                start=True,
-                stop=False,
-            )
-            nc.tensor.matmul_mx(
-                out=acc[:],
-                lhsT=adj_words[:].bitcast(FP8X4),
-                lhsT_scale=adj_plane[:],
-                rhs=y_words[:].bitcast(FP8X4),
-                rhs_scale=y_plane[:],
-                start=False,
-                stop=True,
-            )
+            acc = ps_o.tile([P, C], F32, name="acc")
+            for s in range(2):
+                cols = slice(s * C_DIRECT, C_DIRECT if s == 0 else C)
+                nc.tensor.matmul_mx(
+                    out=acc[:, cols],
+                    lhsT=uv_words[:, b, 0:P].bitcast(FP8X4),
+                    lhsT_scale=uv_plane[:, b, 0:P],
+                    rhs=proj_words[:, cols].bitcast(FP8X4),
+                    rhs_scale=proj_plane[:, cols],
+                    start=True,
+                    stop=False,
+                )
+                nc.tensor.matmul_mx(
+                    out=acc[:, cols],
+                    lhsT=adj_words[:, s, :].bitcast(FP8X4),
+                    lhsT_scale=adj_plane[:, s, :],
+                    rhs=y_words[:, cols].bitcast(FP8X4),
+                    rhs_scale=y_plane[:, cols],
+                    start=False,
+                    stop=True,
+                )
             return acc
 
         def finish(b, acc):
-            result = work.tile([P, C], F32)
+            result = work.tile([P, C], F32, name="result")
             nc.vector.tensor_tensor(out=result[:], in0=acc[:], in1=xpb[:, b, :], op=ADD)
             nc.sync.dma_start(out=out[b], in_=result[:])
 
+        turn_bias()
         spread_bias(0)
+        turned = {}
         first = []
-        for b in range(AHEAD):
-            transpose_streams(b)
+        for b in range(2):
+            turned[b] = transpose_streams(b)
+            copy_streams(b, turned[b])
+            halve_stream(b, turned[b])
             first.append(mix_streams(b))
-        for n in range(1, N_CHUNKS):
-            spread_bias(n)
+        spread_bias(1)
         spread_proj_bias()
-        for b in range(AHEAD):
+        for b in range(2):
             quantise_streams(b, first[b])
-        banks = [graph_matmul(0, n) for n in range(N_CHUNKS)]
+        turned[2] = transpose_streams(2)
+        copy_streams(2, turned[2])
+        halve_stream(2, turned[2])
+        turned[3] = transpose_streams(3)
+        banks = {}
+        for i in range(N_DIRECT):
+            banks[i] = direct_matmul(0, i)
+            banks[N_DIRECT + i] = turned_matmul(0, N_DIRECT + i)
         pending = None
         for b in range(B):
-            if b + AHEAD < B:
-                transpose_streams(b + AHEAD)
-            nc.gpsimd.tensor_tensor(out=xpb[:, b, :], in0=x_sb[:, b, :], in1=projb_all[:], op=ADD)
-            y_ck = work.tile([P, C, K], BF16, align_bytes=64)
-            for n in range(N_CHUNKS):
-                cols = slice(n * CHUNK, (n + 1) * CHUNK)
-                nc.vector.tensor_tensor(
-                    out=y_ck[:, cols, :],
-                    in0=banks[n][:].rearrange("p k c -> p c k"),
-                    in1=bias_ck[:, cols, :],
-                    op=ADD,
-                )
-                if b + 1 < B:
-                    banks[n] = graph_matmul(b + 1, n)
+            more = b + 1 < B
             if pending is not None:
-                finish(b - 1, pending)
-            if b + AHEAD < B:
-                uv_next = mix_streams(b + AHEAD)
-            y_words = work.tile([P, C], U32, align_bytes=64)
-            y_plane = work.tile([P, C], U8, align_bytes=64)
+                acc = output_matmul(b - 1, pending[0], pending[1])
+            nc.gpsimd.tensor_tensor(out=xpb[:, b, :], in0=x_sb[:, b, :], in1=projb_all[:], op=ADD)
+            y_ck = work.tile([P, C, K], BF16, align_bytes=64, name="y_ck")
+            y_t = work.tile([P, N_TURNED, K, P], BF16, name="y_t")
+            direct_bias(y_ck, 0, banks[0])
+            turned_bias_add(y_t, 2, banks[2])
+            if more:
+                banks[0] = direct_matmul(b + 1, 0)
+                banks[2] = turned_matmul(b + 1, 2)
+            direct_bias(y_ck, 1, banks[1])
+            turned_bias_add(y_t, 3, banks[3])
+            back = turn_back(y_t)
+            if b + 4 < B:
+                turned[b + 4] = transpose_streams(b + 4)
+            if more:
+                banks[1] = direct_matmul(b + 1, 1)
+                banks[3] = turned_matmul(b + 1, 3)
+            if b + 3 < B:
+                copy_streams(b + 3, turned[b + 3])
+            if b == 0:
+                interleave_adjacency()
+            copy_back(y_ck, back)
+            if b + 3 < B:
+                halve_stream(b + 3, turned[b + 3])
+            if b + 2 < B:
+                uv_next = mix_streams(b + 2)
+            if pending is not None:
+                finish(b - 1, acc)
+            if b + 2 < B:
+                quantise_streams(b + 2, uv_next)
+            if b == 0:
+                quantise_adjacency()
+            y_words = work.tile([P, C], U32, align_bytes=64, name="y_words")
+            y_plane = work.tile([P, C], U8, align_bytes=64, name="y_plane")
             nc.vector.quantize_mx(
                 out=y_words[:].bitcast(FP8X4),
                 scales=y_plane[:],
                 in_=y_ck[:].rearrange("p c k -> p (c k)"),
             )
-            if b + AHEAD < B:
-                quantise_streams(b + AHEAD, uv_next)
-            if b == 0:
-                quantise_adjacency()
-            pending = output_matmul(b, y_words, y_plane)
-        finish(B - 1, pending)
+            pending = (y_words, y_plane)
+        acc = output_matmul(B - 1, pending[0], pending[1])
+        finish(B - 1, acc)

@@ -59,7 +59,9 @@ def tile_block_pb_kernel(
         x_sb = keep.tile([P, B, C], BF16)
         adj_sb = keep.tile([P, K, P], BF16)
         adj2_sb = keep.tile([P, K, P], BF16)
-        gcn2_words = keep.tile([P, K * C], U32, align_bytes=64)
+        gcn2_words = [
+            keep.tile([P, K, C_DIRECT], U32, align_bytes=64, name="gcn2_words_%d" % s) for s in range(2)
+        ]
         proj_words = keep.tile([P, C], U32, align_bytes=64)
         gcn2_plane = keep.tile([P, K * C], U8, align_bytes=64)
         proj_plane = keep.tile([P, C], U8, align_bytes=64)
@@ -80,9 +82,9 @@ def tile_block_pb_kernel(
         adj_plane = keep.tile([P, 2, P], U8, align_bytes=64)
         xpb = keep.tile([P, B, C], F32)
 
+        nc.vector.memset(gcn2_plane[:].bitcast(I32), 0)
         nc.vector.memset(bias_row[:].bitcast(I32), 0)
         nc.vector.memset(bias_rows[:].bitcast(I32), 0)
-        nc.vector.memset(gcn2_plane[:].bitcast(I32), 0)
         nc.vector.memset(proj_plane[:].bitcast(I32), 0)
         nc.vector.memset(ones[:], 1.0)
         make_identity(nc, ident_f32[:])
@@ -112,10 +114,20 @@ def tile_block_pb_kernel(
                 out=words[:].bitcast(I32), in_=dram[0].rearrange("p n t -> p (n t)").bitcast(I32)
             )
 
+        def load_graph_words(s):
+            nc.sync.dma_start(
+                out=gcn2_words[s][:].bitcast(I32),
+                in_=gcn2_w_words[0]
+                .rearrange("p n t -> p (n t)")
+                .bitcast(I32)
+                .rearrange("p (k c) -> p k c", k=K)[:, :, s * C_DIRECT : (s + 1) * C_DIRECT],
+            )
+
         load_streams(0)
         load_streams(1)
         load_scales(gcn2_plane, gcn2_w_scales)
-        load_words(gcn2_words, gcn2_w_words)
+        load_graph_words(0)
+        load_graph_words(1)
         load_streams(2)
         load_streams(3)
         nc.sync.dma_start(out=adj_sb[:], in_=adj.rearrange("k j w -> j k w"))
@@ -137,7 +149,7 @@ def tile_block_pb_kernel(
                 nc.tensor.matmul(
                     out=bank[:, k, :], lhsT=ones[:], rhs=bias_row[:, cols], start=True, stop=True
                 )
-            nc.scalar.copy(
+            nc.vector.tensor_copy(
                 out=bias_ck[:, n * CHUNK : (n + 1) * CHUNK, :],
                 in_=bank[:].rearrange("p k c -> p c k"),
             )
@@ -178,15 +190,21 @@ def tile_block_pb_kernel(
                 mul=S_G2A,
             )
 
-        def mix_streams(b):
+        def mix_streams(b, halved):
             uv = work.tile([P, 2, C], BF16, align_bytes=64, name="uv")
             nc.vector.scalar_tensor_tensor(
                 out=uv[:, 1, :], in0=ag_t[:, b, 0, :], scalar=S_A2G, in1=ag_t[:, b, 1, :],
                 op0=MULT, op1=ADD,
             )
-            nc.vector.tensor_tensor(
-                out=uv[:, 0, :], in0=ag_t[:, b, 0, :], in1=half_g_t[:, b, :], op=ADD
-            )
+            if halved:
+                nc.vector.tensor_tensor(
+                    out=uv[:, 0, :], in0=ag_t[:, b, 0, :], in1=half_g_t[:, b, :], op=ADD
+                )
+            else:
+                nc.vector.scalar_tensor_tensor(
+                    out=uv[:, 0, :], in0=ag_t[:, b, 1, :], scalar=S_G2A, in1=ag_t[:, b, 0, :],
+                    op0=MULT, op1=ADD,
+                )
             return uv
 
         def quantise_streams(b, uv):
@@ -215,7 +233,7 @@ def tile_block_pb_kernel(
                     out=bank[:, k, :],
                     lhsT=uv_words[:, b, P : 2 * P].bitcast(FP8X4),
                     lhsT_scale=uv_plane[:, b, P : 2 * P],
-                    rhs=gcn2_words[:, cols].bitcast(FP8X4),
+                    rhs=gcn2_words[0][:, k, n * CHUNK : (n + 1) * CHUNK].bitcast(FP8X4),
                     rhs_scale=gcn2_plane[:, cols],
                     start=True,
                     stop=True,
@@ -228,7 +246,9 @@ def tile_block_pb_kernel(
                 cols = slice(k * C + n * CHUNK, k * C + (n + 1) * CHUNK)
                 nc.tensor.matmul_mx(
                     out=bank[:, k, :],
-                    lhsT=gcn2_words[:, cols].bitcast(FP8X4),
+                    lhsT=gcn2_words[1][
+                        :, k, (n - N_DIRECT) * CHUNK : (n - N_DIRECT + 1) * CHUNK
+                    ].bitcast(FP8X4),
                     lhsT_scale=gcn2_plane[:, cols],
                     rhs=uv_words[:, b, P : 2 * P].bitcast(FP8X4),
                     rhs_scale=uv_plane[:, b, P : 2 * P],
@@ -304,61 +324,101 @@ def tile_block_pb_kernel(
             nc.vector.tensor_tensor(out=result[:], in0=acc[:], in1=xpb[:, b, :], op=ADD)
             nc.sync.dma_start(out=out[b], in_=result[:])
 
-        turn_bias()
-        spread_bias(0)
         turned = {}
-        first = []
-        for b in range(2):
-            turned[b] = transpose_streams(b)
-            copy_streams(b, turned[b])
-            halve_stream(b, turned[b])
-            first.append(mix_streams(b))
-        spread_bias(1)
-        spread_proj_bias()
-        for b in range(2):
-            quantise_streams(b, first[b])
-        turned[2] = transpose_streams(2)
-        copy_streams(2, turned[2])
-        halve_stream(2, turned[2])
-        turned[3] = transpose_streams(3)
         banks = {}
-        for i in range(N_DIRECT):
-            banks[i] = direct_matmul(0, i)
-            banks[N_DIRECT + i] = turned_matmul(0, N_DIRECT + i)
+        y_ts = {}
+        backs = {}
+        uvs = {}
+
+        def input_turn(b):
+            if b < B:
+                turned[b] = transpose_streams(b)
+
+        def input_copy(b, halved):
+            if b < B:
+                copy_streams(b, turned[b])
+                if halved:
+                    halve_stream(b, turned[b])
+
+        def mix(b, halved):
+            if b < B:
+                uvs[b] = mix_streams(b, halved)
+
+        def quantise(b):
+            if b < B:
+                quantise_streams(b, uvs[b])
+
+        def direct(b, n):
+            if b < B:
+                banks[n] = direct_matmul(b, n)
+
+        def turned_mm(b, n):
+            if b < B:
+                banks[n] = turned_matmul(b, n)
+
+        def turned_add(b, n):
+            if b < B:
+                if n == N_DIRECT:
+                    y_ts[b] = work.tile([P, N_TURNED, K, P], BF16, name="y_t")
+                turned_bias_add(y_ts[b], n, banks[n])
+
+        def back_turn(b):
+            if b < B:
+                backs[b] = turn_back(y_ts[b])
+
+        turn_bias()
+        spread_proj_bias()
+        spread_bias(0)
+        spread_bias(1)
+        input_turn(0)
+        input_copy(0, False)
+        mix(0, False)
+        quantise(0)
+        input_turn(1)
+        input_copy(1, False)
+        mix(1, False)
+        quantise(1)
+        direct(0, 0)
+        direct(0, 1)
+        turned_mm(0, 2)
+        turned_mm(0, 3)
+        turned_add(0, 2)
+        turned_add(0, 3)
+        input_turn(2)
+        input_turn(3)
+        turned_mm(1, 2)
+        turned_mm(1, 3)
+        back_turn(0)
+        input_copy(2, False)
+        input_copy(3, True)
+        input_turn(4)
         pending = None
         for b in range(B):
-            more = b + 1 < B
             if pending is not None:
                 acc = output_matmul(b - 1, pending[0], pending[1])
             nc.gpsimd.tensor_tensor(out=xpb[:, b, :], in0=x_sb[:, b, :], in1=projb_all[:], op=ADD)
             y_ck = work.tile([P, C, K], BF16, align_bytes=64, name="y_ck")
-            y_t = work.tile([P, N_TURNED, K, P], BF16, name="y_t")
-            direct_bias(y_ck, 0, banks[0])
-            turned_bias_add(y_t, 2, banks[2])
-            if more:
-                banks[0] = direct_matmul(b + 1, 0)
-                banks[2] = turned_matmul(b + 1, 2)
-            direct_bias(y_ck, 1, banks[1])
-            turned_bias_add(y_t, 3, banks[3])
-            back = turn_back(y_t)
-            if b + 4 < B:
-                turned[b + 4] = transpose_streams(b + 4)
-            if more:
-                banks[1] = direct_matmul(b + 1, 1)
-                banks[3] = turned_matmul(b + 1, 3)
-            if b + 3 < B:
-                copy_streams(b + 3, turned[b + 3])
+            copy_back(y_ck, backs[b])
             if b == 0:
                 interleave_adjacency()
-            copy_back(y_ck, back)
-            if b + 3 < B:
-                halve_stream(b + 3, turned[b + 3])
-            if b + 2 < B:
-                uv_next = mix_streams(b + 2)
+            direct_bias(y_ck, 0, banks[0])
+            direct(b + 1, 0)
+            direct_bias(y_ck, 1, banks[1])
+            direct(b + 1, 1)
+            if b == 0:
+                mix(2, False)
+                quantise(2)
+            turned_add(b + 1, 2)
+            turned_mm(b + 2, 2)
+            turned_add(b + 1, 3)
+            turned_mm(b + 2, 3)
+            back_turn(b + 1)
+            input_turn(b + 5)
+            input_copy(b + 4, True)
+            mix(b + 3, True)
             if pending is not None:
                 finish(b - 1, acc)
-            if b + 2 < B:
-                quantise_streams(b + 2, uv_next)
+            quantise(b + 3)
             if b == 0:
                 quantise_adjacency()
             y_words = work.tile([P, C], U32, align_bytes=64, name="y_words")

@@ -14,6 +14,8 @@ MULT = mybir.AluOpType.mult
 IDENTITY = mybir.ActivationFunctionType.Identity
 
 P = 128
+HALF = P // 2
+PACK = 4
 B = 8
 H = 8
 C = 512
@@ -47,15 +49,16 @@ def tile_block_pb_kernel(
     with ExitStack() as ctx:
         keep = ctx.enter_context(tc.tile_pool(name="keep", bufs=1))
         work = ctx.enter_context(tc.tile_pool(name="work", bufs=2))
-        ps_t = ctx.enter_context(tc.psum_pool(name="ps_t", bufs=2))
+        ps_m = ctx.enter_context(tc.psum_pool(name="ps_m", bufs=2))
         ps_yd = ctx.enter_context(tc.psum_pool(name="ps_yd", bufs=N_DIRECT))
         ps_yt = ctx.enter_context(tc.psum_pool(name="ps_yt", bufs=N_TURNED))
         ps_r = ctx.enter_context(tc.psum_pool(name="ps_r", bufs=1))
         ps_o = ctx.enter_context(tc.psum_pool(name="ps_o", bufs=1))
         ctx.enter_context(tc.manual_schedule())
 
-        a_sb = keep.tile([P, B, C], BF16)
-        g_sb = keep.tile([P, B, C], BF16)
+        ag_sb = keep.tile([P, B, 2, C], BF16)
+        mixer = keep.tile([P, P], BF16)
+        mixer_tmp = keep.tile([P, HALF], BF16)
         x_sb = keep.tile([P, B, C], BF16)
         adj_sb = keep.tile([P, K, P], BF16)
         adj2_sb = keep.tile([P, K, P], BF16)
@@ -73,8 +76,6 @@ def tile_block_pb_kernel(
         projb_all = keep.tile([P, C], F32)
         ident_f32 = keep.tile([P, P], F32)
         ident_bf = keep.tile([P, P], BF16)
-        ag_t = keep.tile([P, B, 2, C], BF16)
-        half_g_t = keep.tile([P, B, C], BF16)
         uv_words = keep.tile([P, B, 2 * P], U32, align_bytes=64)
         uv_plane = keep.tile([P, B, 2 * P], U8, align_bytes=64)
         adj_kw = keep.tile([P, 2, P, K], BF16, align_bytes=64)
@@ -87,8 +88,8 @@ def tile_block_pb_kernel(
         nc.vector.memset(bias_rows[:].bitcast(I32), 0)
         nc.vector.memset(proj_plane[:].bitcast(I32), 0)
         nc.vector.memset(ones[:], 1.0)
-        make_identity(nc, ident_f32[:])
         make_identity(nc, ident_bf[:])
+        make_identity(nc, ident_f32[:])
 
         nc.scalar.dma_start(out=bias_row[0:1, 0 : K * C], in_=gcn2_b.unsqueeze(0))
         nc.scalar.dma_start(
@@ -97,11 +98,14 @@ def tile_block_pb_kernel(
         nc.scalar.dma_start(out=bias_row[0:1, K * C : K * C + C], in_=proj_b.unsqueeze(0))
 
         def load_streams(b):
+            for s in range(2):
+                nc.sync.dma_start(
+                    out=ag_sb[0:HALF, b, s, :].rearrange("j (h d) -> j h d", h=H),
+                    in_=attn_o[b, :, s * HALF : (s + 1) * HALF, :].rearrange("h j d -> j h d"),
+                )
             nc.sync.dma_start(
-                out=a_sb[:, b, :].rearrange("j (h d) -> j h d", h=H),
-                in_=attn_o[b].rearrange("h j d -> j h d"),
+                out=ag_sb[HALF:P, b, :, :], in_=xg1[b].rearrange("(s j) c -> j s c", s=2)
             )
-            nc.sync.dma_start(out=g_sb[:, b, :], in_=xg1[b])
 
         def load_scales(plane, scales):
             for r in range(4):
@@ -166,52 +170,47 @@ def tile_block_pb_kernel(
             )
             nc.scalar.copy(out=projb_all[:], in_=acc[:])
 
-        def transpose_streams(b):
-            turned = ps_t.tile([P, 4, P], F32, name="turned")
-            for which, src in enumerate((a_sb, g_sb)):
-                for half in range(2):
-                    nc.tensor.transpose(
-                        out=turned[:, 2 * which + half, :],
-                        in_=src[:, b, :].bitcast(F32)[:, half : C // 2 : 2],
-                        identity=ident_f32[:],
-                    )
-            return turned
-
-        def copy_streams(b, turned):
-            nc.scalar.copy(
-                out=ag_t[:, b].bitcast(F32).rearrange("p x (j h) -> p x j h", h=2),
-                in_=turned[:].rearrange("p (x h) j -> p x j h", h=2),
-            )
-
-        def halve_stream(b, turned):
-            nc.scalar.mul(
-                out=half_g_t[:, b, :].rearrange("p (j h e) -> p j h e", h=2, e=2),
-                in_=turned[:, 2:4, :].bitcast(BF16).rearrange("p h (j e) -> p j h e", e=2),
-                mul=S_G2A,
-            )
-
-        def mix_streams(b, halved):
-            uv = work.tile([P, 2, C], BF16, align_bytes=64, name="uv")
+        def build_mixer():
             nc.vector.scalar_tensor_tensor(
-                out=uv[:, 1, :], in0=ag_t[:, b, 0, :], scalar=S_A2G, in1=ag_t[:, b, 1, :],
+                out=mixer_tmp[:], in0=ident_bf[:, 0:HALF], scalar=2.0, in1=ident_bf[:, HALF:P],
                 op0=MULT, op1=ADD,
             )
-            if halved:
-                nc.vector.tensor_tensor(
-                    out=uv[:, 0, :], in0=ag_t[:, b, 0, :], in1=half_g_t[:, b, :], op=ADD
-                )
+            nc.vector.scalar_tensor_tensor(
+                out=mixer[:, HALF:P], in0=ident_bf[:, HALF:P], scalar=1.0 / S_A2G,
+                in1=ident_bf[:, 0:HALF], op0=MULT, op1=ADD,
+            )
+            nc.vector.tensor_scalar_mul(
+                out=mixer[:, 0:HALF], in0=mixer_tmp[:], scalar1=S_G2A / S_A2G
+            )
+
+        def mix_matmul(b):
+            halves = []
+            for s in range(2):
+                mixed = ps_m.tile([P, 2, PACK, HALF], F32, name="mixed")
+                for t in range(PACK):
+                    nc.tensor.matmul(
+                        out=mixed[:, :, t, :],
+                        lhsT=ag_sb[:, b, s, t:C:PACK],
+                        rhs=mixer[:],
+                        start=True,
+                        stop=True,
+                    )
+                halves.append(mixed)
+            return halves
+
+        def mix_copy(uv, s, mixed, on_vector):
+            dst = uv[:, :, s * HALF : (s + 1) * HALF, :]
+            src = mixed[:].rearrange("p x t j -> p x j t")
+            if on_vector:
+                nc.vector.tensor_scalar_mul(out=dst, in0=src, scalar1=S_A2G)
             else:
-                nc.vector.scalar_tensor_tensor(
-                    out=uv[:, 0, :], in0=ag_t[:, b, 1, :], scalar=S_G2A, in1=ag_t[:, b, 0, :],
-                    op0=MULT, op1=ADD,
-                )
-            return uv
+                nc.scalar.mul(out=dst, in_=src, mul=S_A2G)
 
         def quantise_streams(b, uv):
             nc.vector.quantize_mx(
                 out=uv_words[:, b, :].bitcast(FP8X4),
                 scales=uv_plane[:, b, :],
-                in_=uv[:].rearrange("p s c -> p (s c)"),
+                in_=uv[:].rearrange("p x j t -> p (x j t)"),
             )
 
         def interleave_adjacency():
@@ -324,25 +323,22 @@ def tile_block_pb_kernel(
             nc.vector.tensor_tensor(out=result[:], in0=acc[:], in1=xpb[:, b, :], op=ADD)
             nc.sync.dma_start(out=out[b], in_=result[:])
 
-        turned = {}
+        mixeds = {}
         banks = {}
         y_ts = {}
         backs = {}
         uvs = {}
+        y_cks = {}
 
-        def input_turn(b):
+        def mix(b):
             if b < B:
-                turned[b] = transpose_streams(b)
+                mixeds[b] = mix_matmul(b)
 
-        def input_copy(b, halved):
+        def mix_out(b, shared):
             if b < B:
-                copy_streams(b, turned[b])
-                if halved:
-                    halve_stream(b, turned[b])
-
-        def mix(b, halved):
-            if b < B:
-                uvs[b] = mix_streams(b, halved)
+                uvs[b] = work.tile([P, 2, P, PACK], BF16, align_bytes=64, name="uv")
+                mix_copy(uvs[b], 0, mixeds[b][0], False)
+                mix_copy(uvs[b], 1, mixeds[b][1], shared)
 
         def quantise(b):
             if b < B:
@@ -366,68 +362,78 @@ def tile_block_pb_kernel(
             if b < B:
                 backs[b] = turn_back(y_ts[b])
 
-        turn_bias()
-        spread_proj_bias()
-        spread_bias(0)
-        spread_bias(1)
-        input_turn(0)
-        input_copy(0, False)
-        mix(0, False)
-        quantise(0)
-        input_turn(1)
-        input_copy(1, False)
-        mix(1, False)
-        quantise(1)
-        direct(0, 0)
-        direct(0, 1)
-        turned_mm(0, 2)
-        turned_mm(0, 3)
-        turned_add(0, 2)
-        turned_add(0, 3)
-        input_turn(2)
-        input_turn(3)
-        turned_mm(1, 2)
-        turned_mm(1, 3)
-        back_turn(0)
-        input_copy(2, False)
-        input_copy(3, True)
-        input_turn(4)
-        pending = None
-        for b in range(B):
-            if pending is not None:
-                acc = output_matmul(b - 1, pending[0], pending[1])
+        def add_residual_bias(b):
             nc.gpsimd.tensor_tensor(out=xpb[:, b, :], in0=x_sb[:, b, :], in1=projb_all[:], op=ADD)
-            y_ck = work.tile([P, C, K], BF16, align_bytes=64, name="y_ck")
-            copy_back(y_ck, backs[b])
-            if b == 0:
-                interleave_adjacency()
-            direct_bias(y_ck, 0, banks[0])
-            direct(b + 1, 0)
-            direct_bias(y_ck, 1, banks[1])
-            direct(b + 1, 1)
-            if b == 0:
-                mix(2, False)
-                quantise(2)
-            turned_add(b + 1, 2)
-            turned_mm(b + 2, 2)
-            turned_add(b + 1, 3)
-            turned_mm(b + 2, 3)
-            back_turn(b + 1)
-            input_turn(b + 5)
-            input_copy(b + 4, True)
-            mix(b + 3, True)
-            if pending is not None:
-                finish(b - 1, acc)
-            quantise(b + 3)
-            if b == 0:
-                quantise_adjacency()
+
+        def quantise_y(b):
             y_words = work.tile([P, C], U32, align_bytes=64, name="y_words")
             y_plane = work.tile([P, C], U8, align_bytes=64, name="y_plane")
             nc.vector.quantize_mx(
                 out=y_words[:].bitcast(FP8X4),
                 scales=y_plane[:],
-                in_=y_ck[:].rearrange("p c k -> p (c k)"),
+                in_=y_cks[b][:].rearrange("p c k -> p (c k)"),
             )
-            pending = (y_words, y_plane)
+            return (y_words, y_plane)
+
+        build_mixer()
+        turn_bias()
+        spread_proj_bias()
+        spread_bias(0)
+        spread_bias(1)
+        for b in range(2):
+            mix(b)
+            mix_out(b, True)
+            quantise(b)
+        direct(0, 0)
+        direct(0, 1)
+        turned_mm(0, 2)
+        turned_mm(0, 3)
+        add_residual_bias(0)
+        y_cks[0] = work.tile([P, C, K], BF16, align_bytes=64, name="y_ck")
+        direct_bias(y_cks[0], 0, banks[0])
+        direct_bias(y_cks[0], 1, banks[1])
+        turned_add(0, 2)
+        turned_add(0, 3)
+        mix(2)
+        direct(1, 0)
+        direct(1, 1)
+        mix_out(2, True)
+        quantise(2)
+        turned_mm(1, 2)
+        turned_mm(1, 3)
+        back_turn(0)
+        copy_back(y_cks[0], backs[0])
+        interleave_adjacency()
+        mix(3)
+        mix_out(3, True)
+        quantise(3)
+        turned_add(1, 2)
+        turned_mm(2, 2)
+        turned_add(1, 3)
+        turned_mm(2, 3)
+        back_turn(1)
+        mix(4)
+        mix_out(4, False)
+        quantise_adjacency()
+        pending = quantise_y(0)
+        for b in range(1, B):
+            acc = output_matmul(b - 1, pending[0], pending[1])
+            mix(b + 4)
+            add_residual_bias(b)
+            y_cks[b] = work.tile([P, C, K], BF16, align_bytes=64, name="y_ck")
+            copy_back(y_cks[b], backs[b])
+            direct_bias(y_cks[b], 0, banks[0])
+            direct(b + 1, 0)
+            direct_bias(y_cks[b], 1, banks[1])
+            direct(b + 1, 1)
+            turned_add(b + 1, 2)
+            turned_mm(b + 2, 2)
+            turned_add(b + 1, 3)
+            turned_mm(b + 2, 3)
+            back_turn(b + 1)
+            mix_out(b + 4, False)
+            finish(b - 1, acc)
+            quantise(b + 3)
+            pending = quantise_y(b)
         acc = output_matmul(B - 1, pending[0], pending[1])
         finish(B - 1, acc)

@@ -127,24 +127,32 @@ def tile_block_pb_kernel(
                 .rearrange("p (k c) -> p k c", k=K)[:, :, s * C_DIRECT : (s + 1) * C_DIRECT],
             )
 
+        def load_residual(b):
+            nc.sync.dma_start(out=x_sb[:, b, :], in_=x[b])
+
         load_streams(0)
         load_streams(1)
         load_scales(gcn2_plane, gcn2_w_scales)
-        load_graph_words(0)
         load_graph_words(1)
-        load_streams(2)
-        load_streams(3)
+        load_graph_words(0)
         nc.sync.dma_start(out=adj_sb[:], in_=adj.rearrange("k j w -> j k w"))
         nc.sync.dma_start(
             out=adj2_sb[:].rearrange("p (u e) w -> p u e w", u=2),
             in_=adj.rearrange("k j w -> (k j) w").rearrange("(u p e) w -> p u e w", u=2, e=2),
         )
+        load_streams(2)
         load_scales(proj_plane, proj_w_scales)
         load_words(proj_words, proj_w_words)
-        for b in range(B):
-            if b + 4 < B:
-                load_streams(b + 4)
-            nc.sync.dma_start(out=x_sb[:, b, :], in_=x[b])
+        load_streams(3)
+        load_residual(0)
+        load_streams(4)
+        load_streams(5)
+        load_residual(1)
+        load_streams(6)
+        load_residual(2)
+        load_streams(7)
+        for b in range(3, B):
+            load_residual(b)
 
         def spread_bias(n):
             bank = ps_yd.tile([P, K, CHUNK], F32, name="bank_d")
@@ -375,6 +383,11 @@ def tile_block_pb_kernel(
             )
             return (y_words, y_plane)
 
+        def new_y(b):
+            y_cks[b] = work.tile([P, C, K], BF16, align_bytes=64, name="y_ck")
+
+        pend = {}
+        accs = {}
         build_mixer()
         turn_bias()
         spread_proj_bias()
@@ -384,56 +397,68 @@ def tile_block_pb_kernel(
             mix(b)
             mix_out(b, True)
             quantise(b)
-        direct(0, 0)
-        direct(0, 1)
         turned_mm(0, 2)
         turned_mm(0, 3)
-        add_residual_bias(0)
-        y_cks[0] = work.tile([P, C, K], BF16, align_bytes=64, name="y_ck")
-        direct_bias(y_cks[0], 0, banks[0])
-        direct_bias(y_cks[0], 1, banks[1])
+        direct(0, 0)
+        direct(0, 1)
         turned_add(0, 2)
         turned_add(0, 3)
-        mix(2)
-        direct(1, 0)
-        direct(1, 1)
-        mix_out(2, True)
-        quantise(2)
+        add_residual_bias(0)
+        back_turn(0)
         turned_mm(1, 2)
         turned_mm(1, 3)
-        back_turn(0)
-        copy_back(y_cks[0], backs[0])
         interleave_adjacency()
-        mix(3)
-        mix_out(3, True)
-        quantise(3)
+        new_y(0)
+        copy_back(y_cks[0], backs[0])
+        direct_bias(y_cks[0], 0, banks[0])
+        direct_bias(y_cks[0], 1, banks[1])
+        direct(1, 0)
+        direct(1, 1)
+        mix(2)
         turned_add(1, 2)
-        turned_mm(2, 2)
         turned_add(1, 3)
-        turned_mm(2, 3)
-        back_turn(1)
-        mix(4)
-        mix_out(4, False)
+        mix_out(2, False)
+        pend[0] = quantise_y(0)
         quantise_adjacency()
-        pending = quantise_y(0)
-        for b in range(1, B):
-            acc = output_matmul(b - 1, pending[0], pending[1])
-            mix(b + 4)
+        add_residual_bias(1)
+        accs[0] = output_matmul(0, pend[0][0], pend[0][1])
+        mix(3)
+        back_turn(1)
+        new_y(1)
+        direct_bias(y_cks[1], 0, banks[0])
+        direct_bias(y_cks[1], 1, banks[1])
+        quantise(2)
+        turned_mm(2, 2)
+        turned_mm(2, 3)
+        mix_out(3, False)
+        mix(4)
+        direct(2, 0)
+        direct(2, 1)
+        copy_back(y_cks[1], backs[1])
+        turned_add(2, 2)
+        turned_add(2, 3)
+        mix_out(4, False)
+        finish(0, accs[0])
+        quantise(3)
+        pend[1] = quantise_y(1)
+        for b in range(2, B):
             add_residual_bias(b)
-            y_cks[b] = work.tile([P, C, K], BF16, align_bytes=64, name="y_ck")
+            back_turn(b)
+            turned_mm(b + 1, 2)
+            turned_mm(b + 1, 3)
+            accs[b - 1] = output_matmul(b - 1, pend[b - 1][0], pend[b - 1][1])
+            mix(b + 3)
+            new_y(b)
             copy_back(y_cks[b], backs[b])
             direct_bias(y_cks[b], 0, banks[0])
-            direct(b + 1, 0)
             direct_bias(y_cks[b], 1, banks[1])
+            direct(b + 1, 0)
             direct(b + 1, 1)
             turned_add(b + 1, 2)
-            turned_mm(b + 2, 2)
             turned_add(b + 1, 3)
-            turned_mm(b + 2, 3)
-            back_turn(b + 1)
-            mix_out(b + 4, False)
-            finish(b - 1, acc)
-            quantise(b + 3)
-            pending = quantise_y(b)
-        acc = output_matmul(B - 1, pending[0], pending[1])
-        finish(B - 1, acc)
+            mix_out(b + 3, False)
+            quantise(b + 2)
+            pend[b] = quantise_y(b)
+            finish(b - 1, accs[b - 1])
+        accs[B - 1] = output_matmul(B - 1, pend[B - 1][0], pend[B - 1][1])
+        finish(B - 1, accs[B - 1])

@@ -222,8 +222,11 @@ def tile_block_pb_kernel(
             )
 
         def interleave_adjacency():
-            nc.scalar.copy(out=adj_kw[:, 0], in_=adj_sb[:].rearrange("p k w -> p w k"))
-            nc.scalar.copy(out=adj_kw[:, 1], in_=adj2_sb[:].rearrange("p k w -> p w k"))
+            for s, src in enumerate((adj_sb, adj2_sb)):
+                nc.gpsimd.tensor_scalar(
+                    out=adj_kw[:, s], in0=src[:].rearrange("p k w -> p w k"),
+                    scalar1=1.0, scalar2=0.0, op0=MULT, op1=ADD,
+                )
 
         def quantise_adjacency():
             nc.vector.quantize_mx(
@@ -302,34 +305,49 @@ def tile_block_pb_kernel(
                 in_=back[:].rearrange("p i u c -> p i c u"),
             )
 
+        def half_cols(s):
+            return slice(s * C_DIRECT, (s + 1) * C_DIRECT)
+
+        def output_half(acc_half, b, s, y_words, y_plane):
+            cols = half_cols(s)
+            nc.tensor.matmul_mx(
+                out=acc_half,
+                lhsT=uv_words[:, b, 0:P].bitcast(FP8X4),
+                lhsT_scale=uv_plane[:, b, 0:P],
+                rhs=proj_words[:, cols].bitcast(FP8X4),
+                rhs_scale=proj_plane[:, cols],
+                start=True,
+                stop=False,
+            )
+            nc.tensor.matmul_mx(
+                out=acc_half,
+                lhsT=adj_words[:, s, :].bitcast(FP8X4),
+                lhsT_scale=adj_plane[:, s, :],
+                rhs=y_words[:, cols].bitcast(FP8X4),
+                rhs_scale=y_plane[:, cols],
+                start=False,
+                stop=True,
+            )
+
         def output_matmul(b, y_words, y_plane):
-            acc = ps_o.tile([P, C], F32, name="acc")
+            if b + 4 < B:
+                acc = ps_o.tile([P, C], F32, name="acc")
+            else:
+                acc = ps_m.tile([P, C], F32, name="mixed")
             for s in range(2):
-                cols = slice(s * C_DIRECT, C_DIRECT if s == 0 else C)
-                nc.tensor.matmul_mx(
-                    out=acc[:, cols],
-                    lhsT=uv_words[:, b, 0:P].bitcast(FP8X4),
-                    lhsT_scale=uv_plane[:, b, 0:P],
-                    rhs=proj_words[:, cols].bitcast(FP8X4),
-                    rhs_scale=proj_plane[:, cols],
-                    start=True,
-                    stop=False,
-                )
-                nc.tensor.matmul_mx(
-                    out=acc[:, cols],
-                    lhsT=adj_words[:, s, :].bitcast(FP8X4),
-                    lhsT_scale=adj_plane[:, s, :],
-                    rhs=y_words[:, cols].bitcast(FP8X4),
-                    rhs_scale=y_plane[:, cols],
-                    start=False,
-                    stop=True,
-                )
+                output_half(acc[:, half_cols(s)], b, s, y_words, y_plane)
             return acc
 
         def finish(b, acc):
             result = work.tile([P, C], F32, name="result")
             nc.vector.tensor_tensor(out=result[:], in0=acc[:], in1=xpb[:, b, :], op=ADD)
             nc.sync.dma_start(out=out[b], in_=result[:])
+
+        def finish_half(b, s, acc_half):
+            cols = half_cols(s)
+            result = work.tile([P, C_DIRECT], F32, name="result_half")
+            nc.vector.tensor_tensor(out=result[:], in0=acc_half[:], in1=xpb[:, b, cols], op=ADD)
+            nc.sync.dma_start(out=out[b, :, cols], in_=result[:])
 
         mixeds = {}
         banks = {}
@@ -383,6 +401,25 @@ def tile_block_pb_kernel(
             )
             return (y_words, y_plane)
 
+        def last_batch_in_halves(b):
+            y_words = work.tile([P, C], U32, align_bytes=64, name="y_words")
+            y_plane = work.tile([P, C], U8, align_bytes=64, name="y_plane")
+            acc_halves = [
+                ps_m.tile([P, C_DIRECT], F32, name="mixed"),
+                ps_o.tile([P, C_DIRECT], F32, name="acc"),
+            ]
+            for s in range(2):
+                cols = half_cols(s)
+                nc.vector.quantize_mx(
+                    out=y_words[:, cols].bitcast(FP8X4),
+                    scales=y_plane[:, cols],
+                    in_=y_cks[b][:, cols, :].rearrange("p c k -> p (c k)"),
+                )
+                output_half(acc_halves[s][:], b, s, y_words, y_plane)
+            finish(b - 1, accs[b - 1])
+            for s in range(2):
+                finish_half(b, s, acc_halves[s])
+
         def new_y(b):
             y_cks[b] = work.tile([P, C, K], BF16, align_bytes=64, name="y_ck")
 
@@ -403,11 +440,11 @@ def tile_block_pb_kernel(
         direct(0, 1)
         turned_add(0, 2)
         turned_add(0, 3)
+        interleave_adjacency()
         add_residual_bias(0)
         back_turn(0)
         turned_mm(1, 2)
         turned_mm(1, 3)
-        interleave_adjacency()
         new_y(0)
         copy_back(y_cks[0], backs[0])
         direct_bias(y_cks[0], 0, banks[0])
@@ -458,7 +495,7 @@ def tile_block_pb_kernel(
             turned_add(b + 1, 3)
             mix_out(b + 3, False)
             quantise(b + 2)
-            pend[b] = quantise_y(b)
-            finish(b - 1, accs[b - 1])
-        accs[B - 1] = output_matmul(B - 1, pend[B - 1][0], pend[B - 1][1])
-        finish(B - 1, accs[B - 1])
+            if b + 1 < B:
+                pend[b] = quantise_y(b)
+                finish(b - 1, accs[b - 1])
+        last_batch_in_halves(B - 1)

@@ -343,6 +343,13 @@ def tile_block_pb_kernel(
             nc.vector.tensor_tensor(out=result[:], in0=acc[:], in1=xpb[:, b, :], op=ADD)
             nc.sync.dma_start(out=out[b], in_=result[:])
 
+        def finish_beside_vector(b, acc):
+            raw = work.tile([P, C], F32, name="raw")
+            nc.scalar.copy(out=raw[:], in_=acc[:])
+            result = work.tile([P, C], F32, name="result")
+            nc.gpsimd.tensor_tensor(out=result[:], in0=raw[:], in1=xpb[:, b, :], op=ADD)
+            nc.sync.dma_start(out=out[b], in_=result[:])
+
         def finish_half(b, s, acc_half):
             cols = half_cols(s)
             result = work.tile([P, C_DIRECT], F32, name="result_half")
@@ -441,7 +448,8 @@ def tile_block_pb_kernel(
         turned_add(0, 2)
         turned_add(0, 3)
         interleave_adjacency()
-        add_residual_bias(0)
+        for b in range(B):
+            add_residual_bias(b)
         back_turn(0)
         turned_mm(1, 2)
         turned_mm(1, 3)
@@ -457,7 +465,6 @@ def tile_block_pb_kernel(
         mix_out(2, False)
         pend[0] = quantise_y(0)
         quantise_adjacency()
-        add_residual_bias(1)
         accs[0] = output_matmul(0, pend[0][0], pend[0][1])
         mix(3)
         back_turn(1)
@@ -479,23 +486,36 @@ def tile_block_pb_kernel(
         quantise(3)
         pend[1] = quantise_y(1)
         for b in range(2, B):
-            add_residual_bias(b)
-            back_turn(b)
-            turned_mm(b + 1, 2)
-            turned_mm(b + 1, 3)
-            accs[b - 1] = output_matmul(b - 1, pend[b - 1][0], pend[b - 1][1])
-            mix(b + 3)
+            draining = b + 2 >= B
             new_y(b)
-            copy_back(y_cks[b], backs[b])
+            if draining:
+                turned_mm(b + 1, 2)
+                back_turn(b)
+                turned_mm(b + 1, 3)
+                turned_add(b + 1, 2)
+                copy_back(y_cks[b], backs[b])
+                turned_add(b + 1, 3)
+            else:
+                back_turn(b)
+                turned_mm(b + 1, 2)
+                turned_mm(b + 1, 3)
+            accs[b - 1] = output_matmul(b - 1, pend[b - 1][0], pend[b - 1][1])
+            if b + 2 == B:
+                finish_beside_vector(b - 1, accs[b - 1])
+            mix(b + 3)
+            if not draining:
+                copy_back(y_cks[b], backs[b])
             direct_bias(y_cks[b], 0, banks[0])
             direct_bias(y_cks[b], 1, banks[1])
             direct(b + 1, 0)
             direct(b + 1, 1)
-            turned_add(b + 1, 2)
-            turned_add(b + 1, 3)
+            if not draining:
+                turned_add(b + 1, 2)
+                turned_add(b + 1, 3)
             mix_out(b + 3, False)
             quantise(b + 2)
             if b + 1 < B:
                 pend[b] = quantise_y(b)
-                finish(b - 1, accs[b - 1])
+                if b + 2 != B:
+                    finish(b - 1, accs[b - 1])
         last_batch_in_halves(B - 1)

from contextlib import ExitStack

import concourse.mybir as mybir
from concourse.masks import make_identity

BF16 = mybir.dt.bfloat16
F32 = mybir.dt.float32
I32 = mybir.dt.int32
U32 = mybir.dt.uint32
U8 = mybir.dt.uint8
FP8X4 = mybir.dt.float8_e4m3fn_x4
ADD = mybir.AluOpType.add
MULT = mybir.AluOpType.mult
IDENTITY = mybir.ActivationFunctionType.Identity

P = 128
HALF = P // 2
PACK = 4
B = 8
H = 8
C = 512
K = 4
CHUNK = 128
N_CHUNKS = C // CHUNK
N_DIRECT = 2
N_TURNED = N_CHUNKS - N_DIRECT
C_DIRECT = N_DIRECT * CHUNK
S_G2A = 0.5
S_A2G = 0.8

FLOPS = 2 * B * P * C * C + 2 * B * P * C * K * C + 2 * B * P * K * P * C


def tile_block_pb_kernel(
    tc,
    attn_o,
    xg1,
    x,
    adj,
    proj_w_words,
    proj_w_scales,
    proj_b,
    gcn2_w_words,
    gcn2_w_scales,
    gcn2_b,
    out,
):
    nc = tc.nc
    with ExitStack() as ctx:
        keep = ctx.enter_context(tc.tile_pool(name="keep", bufs=1))
        work = ctx.enter_context(tc.tile_pool(name="work", bufs=2))
        ps_m = ctx.enter_context(tc.psum_pool(name="ps_m", bufs=2))
        ps_yd = ctx.enter_context(tc.psum_pool(name="ps_yd", bufs=N_DIRECT))
        ps_yt = ctx.enter_context(tc.psum_pool(name="ps_yt", bufs=N_TURNED))
        ps_r = ctx.enter_context(tc.psum_pool(name="ps_r", bufs=1))
        ps_o = ctx.enter_context(tc.psum_pool(name="ps_o", bufs=1))
        ctx.enter_context(tc.manual_schedule())

        ag_sb = keep.tile([P, B, 2, C], BF16)
        mixer = keep.tile([P, P], BF16)
        mixer_tmp = keep.tile([P, HALF], BF16)
        x_sb = keep.tile([P, B, C], BF16)
        adj_sb = keep.tile([P, K, P], BF16)
        adj2_sb = keep.tile([P, K, P], BF16)
        gcn2_words = [
            keep.tile([P, K, C_DIRECT], U32, align_bytes=64, name="gcn2_words_%d" % s) for s in range(2)
        ]
        proj_words = keep.tile([P, C], U32, align_bytes=64)
        gcn2_plane = keep.tile([P, K * C], U8, align_bytes=64)
        proj_plane = keep.tile([P, C], U8, align_bytes=64)
        bias_row = keep.tile([P, K * C + C], BF16)
        bias_rows = keep.tile([P, P], BF16)
        ones = keep.tile([P, P], BF16)
        bias_ck = keep.tile([P, C_DIRECT, K], F32)
        bias_col = keep.tile([P, K * N_CHUNKS], F32)
        projb_all = keep.tile([P, C], F32)
        ident_f32 = keep.tile([P, P], F32)
        ident_bf = keep.tile([P, P], BF16)
        uv_words = keep.tile([P, B, 2 * P], U32, align_bytes=64)
        uv_plane = keep.tile([P, B, 2 * P], U8, align_bytes=64)
        adj_kw = keep.tile([P, 2, P, K], BF16, align_bytes=64)
        adj_words = keep.tile([P, 2, P], U32, align_bytes=64)
        adj_plane = keep.tile([P, 2, P], U8, align_bytes=64)
        xpb = keep.tile([P, B, C], F32)

        nc.vector.memset(gcn2_plane[:].bitcast(I32), 0)
        nc.vector.memset(bias_row[:].bitcast(I32), 0)
        nc.vector.memset(bias_rows[:].bitcast(I32), 0)
        nc.vector.memset(proj_plane[:].bitcast(I32), 0)
        nc.vector.memset(ones[:], 1.0)
        make_identity(nc, ident_bf[:])
        make_identity(nc, ident_f32[:])

        nc.scalar.dma_start(out=bias_row[0:1, 0 : K * C], in_=gcn2_b.unsqueeze(0))
        nc.scalar.dma_start(
            out=bias_rows[0 : K * N_CHUNKS, :], in_=gcn2_b.rearrange("(q c) -> q c", c=CHUNK)
        )
        nc.scalar.dma_start(out=bias_row[0:1, K * C : K * C + C], in_=proj_b.unsqueeze(0))

        def load_streams(b):
            for s in range(2):
                nc.sync.dma_start(
                    out=ag_sb[0:HALF, b, s, :].rearrange("j (h d) -> j h d", h=H),
                    in_=attn_o[b, :, s * HALF : (s + 1) * HALF, :].rearrange("h j d -> j h d"),
                )
            nc.sync.dma_start(
                out=ag_sb[HALF:P, b, :, :], in_=xg1[b].rearrange("(s j) c -> j s c", s=2)
            )

        def load_scales(plane, scales):
            for r in range(4):
                nc.sync.dma_start(
                    out=plane[r:P:32, :].bitcast(I32), in_=scales[0, r:16:4, :].bitcast(I32)
                )

        def load_words(words, dram):
            nc.sync.dma_start(
                out=words[:].bitcast(I32), in_=dram[0].rearrange("p n t -> p (n t)").bitcast(I32)
            )

        def load_graph_words(s):
            nc.sync.dma_start(
                out=gcn2_words[s][:].bitcast(I32),
                in_=gcn2_w_words[0]
                .rearrange("p n t -> p (n t)")
                .bitcast(I32)
                .rearrange("p (k c) -> p k c", k=K)[:, :, s * C_DIRECT : (s + 1) * C_DIRECT],
            )

        def load_residual(b):
            nc.sync.dma_start(out=x_sb[:, b, :], in_=x[b])

        load_streams(0)
        load_streams(1)
        load_scales(gcn2_plane, gcn2_w_scales)
        load_graph_words(1)
        load_graph_words(0)
        nc.sync.dma_start(out=adj_sb[:], in_=adj.rearrange("k j w -> j k w"))
        nc.sync.dma_start(
            out=adj2_sb[:].rearrange("p (u e) w -> p u e w", u=2),
            in_=adj.rearrange("k j w -> (k j) w").rearrange("(u p e) w -> p u e w", u=2, e=2),
        )
        load_streams(2)
        load_scales(proj_plane, proj_w_scales)
        load_words(proj_words, proj_w_words)
        load_streams(3)
        load_residual(0)
        load_streams(4)
        load_streams(5)
        load_residual(1)
        load_streams(6)
        load_residual(2)
        load_streams(7)
        for b in range(3, B):
            load_residual(b)

        def spread_bias(n):
            bank = ps_yd.tile([P, K, CHUNK], F32, name="bank_d")
            for k in range(K):
                cols = slice(k * C + n * CHUNK, k * C + (n + 1) * CHUNK)
                nc.tensor.matmul(
                    out=bank[:, k, :], lhsT=ones[:], rhs=bias_row[:, cols], start=True, stop=True
                )
            nc.vector.tensor_copy(
                out=bias_ck[:, n * CHUNK : (n + 1) * CHUNK, :],
                in_=bank[:].rearrange("p k c -> p c k"),
            )

        def turn_bias():
            turned_bias = ps_r.tile([P, P], BF16, name="bank_r")
            nc.tensor.transpose(out=turned_bias[:], in_=bias_rows[:], identity=ident_bf[:])
            nc.scalar.copy(out=bias_col[:], in_=turned_bias[:, 0 : K * N_CHUNKS])

        def spread_proj_bias():
            acc = ps_o.tile([P, C], F32, name="acc")
            nc.tensor.matmul(
                out=acc[:], lhsT=ones[:], rhs=bias_row[:, K * C : K * C + C], start=True, stop=True
            )
            nc.scalar.copy(out=projb_all[:], in_=acc[:])

        def build_mixer():
            nc.vector.scalar_tensor_tensor(
                out=mixer_tmp[:], in0=ident_bf[:, 0:HALF], scalar=2.0, in1=ident_bf[:, HALF:P],
                op0=MULT, op1=ADD,
            )
            nc.vector.scalar_tensor_tensor(
                out=mixer[:, HALF:P], in0=ident_bf[:, HALF:P], scalar=1.0 / S_A2G,
                in1=ident_bf[:, 0:HALF], op0=MULT, op1=ADD,
            )
            nc.vector.tensor_scalar_mul(
                out=mixer[:, 0:HALF], in0=mixer_tmp[:], scalar1=S_G2A / S_A2G
            )

        def mix_matmul(b):
            halves = []
            for s in range(2):
                mixed = ps_m.tile([P, 2, PACK, HALF], F32, name="mixed")
                for t in range(PACK):
                    nc.tensor.matmul(
                        out=mixed[:, :, t, :],
                        lhsT=ag_sb[:, b, s, t:C:PACK],
                        rhs=mixer[:],
                        start=True,
                        stop=True,
                    )
                halves.append(mixed)
            return halves

        def mix_copy(uv, s, mixed, on_vector):
            dst = uv[:, :, s * HALF : (s + 1) * HALF, :]
            src = mixed[:].rearrange("p x t j -> p x j t")
            if on_vector:
                nc.vector.tensor_scalar_mul(out=dst, in0=src, scalar1=S_A2G)
            else:
                nc.scalar.mul(out=dst, in_=src, mul=S_A2G)

        def quantise_streams(b, uv):
            nc.vector.quantize_mx(
                out=uv_words[:, b, :].bitcast(FP8X4),
                scales=uv_plane[:, b, :],
                in_=uv[:].rearrange("p x j t -> p (x j t)"),
            )

        def interleave_adjacency():
            for s, src in enumerate((adj_sb, adj2_sb)):
                nc.gpsimd.tensor_scalar(
                    out=adj_kw[:, s], in0=src[:].rearrange("p k w -> p w k"),
                    scalar1=1.0, scalar2=0.0, op0=MULT, op1=ADD,
                )

        def quantise_adjacency():
            nc.vector.quantize_mx(
                out=adj_words[:].rearrange("p s w -> p (s w)").bitcast(FP8X4),
                scales=adj_plane[:].rearrange("p s w -> p (s w)"),
                in_=adj_kw[:].rearrange("p s w k -> p (s w k)"),
            )

        def direct_matmul(b, n):
            bank = ps_yd.tile([P, K, CHUNK], F32, name="bank_d")
            for k in range(K):
                cols = slice(k * C + n * CHUNK, k * C + (n + 1) * CHUNK)
                nc.tensor.matmul_mx(
                    out=bank[:, k, :],
                    lhsT=uv_words[:, b, P : 2 * P].bitcast(FP8X4),
                    lhsT_scale=uv_plane[:, b, P : 2 * P],
                    rhs=gcn2_words[0][:, k, n * CHUNK : (n + 1) * CHUNK].bitcast(FP8X4),
                    rhs_scale=gcn2_plane[:, cols],
                    start=True,
                    stop=True,
                )
            return bank

        def turned_matmul(b, n):
            bank = ps_yt.tile([P, K, P], F32, name="bank_t")
            for k in range(K):
                cols = slice(k * C + n * CHUNK, k * C + (n + 1) * CHUNK)
                nc.tensor.matmul_mx(
                    out=bank[:, k, :],
                    lhsT=gcn2_words[1][
                        :, k, (n - N_DIRECT) * CHUNK : (n - N_DIRECT + 1) * CHUNK
                    ].bitcast(FP8X4),
                    lhsT_scale=gcn2_plane[:, cols],
                    rhs=uv_words[:, b, P : 2 * P].bitcast(FP8X4),
                    rhs_scale=uv_plane[:, b, P : 2 * P],
                    start=True,
                    stop=True,
                )
            return bank

        def direct_bias(y_ck, n, bank):
            cols = slice(n * CHUNK, (n + 1) * CHUNK)
            nc.vector.tensor_tensor(
                out=y_ck[:, cols, :],
                in0=bank[:].rearrange("p k c -> p c k"),
                in1=bias_ck[:, cols, :],
                op=ADD,
            )

        def turned_bias_add(y_t, n, bank):
            for k in range(K):
                q = k * N_CHUNKS + n
                nc.scalar.activation(
                    out=y_t[:, n - N_DIRECT, k, :],
                    in_=bank[:, k, :],
                    func=IDENTITY,
                    bias=bias_col[:, q : q + 1],
                )

        def turn_back(y_t):
            back = ps_r.tile([P, N_TURNED, 2, P], F32, name="bank_r")
            for i in range(N_TURNED):
                words = y_t[:, i].rearrange("p k j -> p (k j)").bitcast(F32)
                for u in range(2):
                    nc.tensor.transpose(
                        out=back[:, i, u, :], in_=words[:, u * P : (u + 1) * P], identity=ident_f32[:]
                    )
            return back

        def copy_back(y_ck, back):
            nc.scalar.copy(
                out=y_ck[:, C_DIRECT:C, :]
                .rearrange("p c k -> p (c k)")
                .bitcast(F32)
                .rearrange("p (i c u) -> p i c u", i=N_TURNED, u=2),
                in_=back[:].rearrange("p i u c -> p i c u"),
            )

        def half_cols(s):
            return slice(s * C_DIRECT, (s + 1) * C_DIRECT)

        def output_half(acc_half, b, s, y_words, y_plane):
            cols = half_cols(s)
            nc.tensor.matmul_mx(
                out=acc_half,
                lhsT=uv_words[:, b, 0:P].bitcast(FP8X4),
                lhsT_scale=uv_plane[:, b, 0:P],
                rhs=proj_words[:, cols].bitcast(FP8X4),
                rhs_scale=proj_plane[:, cols],
                start=True,
                stop=False,
            )
            nc.tensor.matmul_mx(
                out=acc_half,
                lhsT=adj_words[:, s, :].bitcast(FP8X4),
                lhsT_scale=adj_plane[:, s, :],
                rhs=y_words[:, cols].bitcast(FP8X4),
                rhs_scale=y_plane[:, cols],
                start=False,
                stop=True,
            )

        def output_matmul(b, y_words, y_plane):
            if b + 4 < B:
                acc = ps_o.tile([P, C], F32, name="acc")
            else:
                acc = ps_m.tile([P, C], F32, name="mixed")
            for s in range(2):
                output_half(acc[:, half_cols(s)], b, s, y_words, y_plane)
            return acc

        def finish(b, acc):
            result = work.tile([P, C], F32, name="result")
            nc.vector.tensor_tensor(out=result[:], in0=acc[:], in1=xpb[:, b, :], op=ADD)
            nc.sync.dma_start(out=out[b], in_=result[:])

        def finish_beside_vector(b, acc):
            raw = work.tile([P, C], F32, name="raw")
            nc.scalar.copy(out=raw[:], in_=acc[:])
            result = work.tile([P, C], F32, name="result")
            nc.gpsimd.tensor_tensor(out=result[:], in0=raw[:], in1=xpb[:, b, :], op=ADD)
            nc.sync.dma_start(out=out[b], in_=result[:])

        def finish_half(b, s, acc_half):
            cols = half_cols(s)
            result = work.tile([P, C_DIRECT], F32, name="result_half")
            nc.vector.tensor_tensor(out=result[:], in0=acc_half[:], in1=xpb[:, b, cols], op=ADD)
            nc.sync.dma_start(out=out[b, :, cols], in_=result[:])

        mixeds = {}
        banks = {}
        y_ts = {}
        backs = {}
        uvs = {}
        y_cks = {}

        def mix(b):
            if b < B:
                mixeds[b] = mix_matmul(b)

        def mix_out(b, shared):
            if b < B:
                uvs[b] = work.tile([P, 2, P, PACK], BF16, align_bytes=64, name="uv")
                mix_copy(uvs[b], 0, mixeds[b][0], False)
                mix_copy(uvs[b], 1, mixeds[b][1], shared)

        def quantise(b):
            if b < B:
                quantise_streams(b, uvs[b])

        def direct(b, n):
            if b < B:
                banks[n] = direct_matmul(b, n)

        def turned_mm(b, n):
            if b < B:
                banks[n] = turned_matmul(b, n)

        def turned_add(b, n):
            if b < B:
                if n == N_DIRECT:
                    y_ts[b] = work.tile([P, N_TURNED, K, P], BF16, name="y_t")
                turned_bias_add(y_ts[b], n, banks[n])

        def back_turn(b):
            if b < B:
                backs[b] = turn_back(y_ts[b])

        def add_residual_bias(b):
            nc.gpsimd.tensor_tensor(out=xpb[:, b, :], in0=x_sb[:, b, :], in1=projb_all[:], op=ADD)

        def quantise_y(b):
            y_words = work.tile([P, C], U32, align_bytes=64, name="y_words")
            y_plane = work.tile([P, C], U8, align_bytes=64, name="y_plane")
            nc.vector.quantize_mx(
                out=y_words[:].bitcast(FP8X4),
                scales=y_plane[:],
                in_=y_cks[b][:].rearrange("p c k -> p (c k)"),
            )
            return (y_words, y_plane)

        def last_batch_in_halves(b):
            y_words = work.tile([P, C], U32, align_bytes=64, name="y_words")
            y_plane = work.tile([P, C], U8, align_bytes=64, name="y_plane")
            acc_halves = [
                ps_m.tile([P, C_DIRECT], F32, name="mixed"),
                ps_o.tile([P, C_DIRECT], F32, name="acc"),
            ]
            for s in range(2):
                cols = half_cols(s)
                nc.vector.quantize_mx(
                    out=y_words[:, cols].bitcast(FP8X4),
                    scales=y_plane[:, cols],
                    in_=y_cks[b][:, cols, :].rearrange("p c k -> p (c k)"),
                )
                output_half(acc_halves[s][:], b, s, y_words, y_plane)
            finish(b - 1, accs[b - 1])
            for s in range(2):
                finish_half(b, s, acc_halves[s])

        def new_y(b):
            y_cks[b] = work.tile([P, C, K], BF16, align_bytes=64, name="y_ck")

        pend = {}
        accs = {}
        build_mixer()
        turn_bias()
        spread_proj_bias()
        spread_bias(0)
        spread_bias(1)
        for b in range(2):
            mix(b)
            mix_out(b, True)
            quantise(b)
        turned_mm(0, 2)
        turned_mm(0, 3)
        direct(0, 0)
        direct(0, 1)
        turned_add(0, 2)
        turned_add(0, 3)
        interleave_adjacency()
        for b in range(B):
            add_residual_bias(b)
        back_turn(0)
        turned_mm(1, 2)
        turned_mm(1, 3)
        new_y(0)
        copy_back(y_cks[0], backs[0])
        direct_bias(y_cks[0], 0, banks[0])
        direct_bias(y_cks[0], 1, banks[1])
        direct(1, 0)
        direct(1, 1)
        mix(2)
        turned_add(1, 2)
        turned_add(1, 3)
        mix_out(2, False)
        pend[0] = quantise_y(0)
        quantise_adjacency()
        accs[0] = output_matmul(0, pend[0][0], pend[0][1])
        mix(3)
        back_turn(1)
        new_y(1)
        direct_bias(y_cks[1], 0, banks[0])
        direct_bias(y_cks[1], 1, banks[1])
        quantise(2)
        turned_mm(2, 2)
        turned_mm(2, 3)
        mix_out(3, False)
        mix(4)
        direct(2, 0)
        direct(2, 1)
        copy_back(y_cks[1], backs[1])
        turned_add(2, 2)
        turned_add(2, 3)
        mix_out(4, False)
        finish(0, accs[0])
        quantise(3)
        pend[1] = quantise_y(1)
        for b in range(2, B):
            draining = b + 2 >= B
            new_y(b)
            if draining:
                turned_mm(b + 1, 2)
                back_turn(b)
                turned_mm(b + 1, 3)
                turned_add(b + 1, 2)
                copy_back(y_cks[b], backs[b])
                turned_add(b + 1, 3)
            else:
                back_turn(b)
                turned_mm(b + 1, 2)
                turned_mm(b + 1, 3)
            accs[b - 1] = output_matmul(b - 1, pend[b - 1][0], pend[b - 1][1])
            if b + 2 == B:
                finish_beside_vector(b - 1, accs[b - 1])
            mix(b + 3)
            if not draining:
                copy_back(y_cks[b], backs[b])
            direct_bias(y_cks[b], 0, banks[0])
            direct_bias(y_cks[b], 1, banks[1])
            direct(b + 1, 0)
            direct(b + 1, 1)
            if not draining:
                turned_add(b + 1, 2)
                turned_add(b + 1, 3)
            mix_out(b + 3, False)
            quantise(b + 2)
            if b + 1 < B:
                pend[b] = quantise_y(b)
                if b + 2 != B:
                    finish(b - 1, accs[b - 1])
        last_batch_in_halves(B - 1)
